import numpy as np
import ml_dtypes


def mxq(x, axis, fmt="e4m3"):
    dtype, down = {"e4m3": (ml_dtypes.float8_e4m3fn, 7), "e5m2": (ml_dtypes.float8_e5m2, 14)}[fmt]
    v = np.moveaxis(np.asarray(x, np.float32).astype(ml_dtypes.bfloat16).astype(np.float64), axis, -1)
    blocks = v.reshape(v.shape[:-1] + (-1, 32))
    amax = np.abs(blocks).max(-1, keepdims=True)
    byte = np.maximum(np.where(amax > 0, np.frexp(amax)[1] - 1 + 127, 0) - down, 1)
    scale = np.exp2(byte - 127.0)
    codes = (blocks / scale).astype(np.float32).astype(dtype).astype(np.float64)
    return np.moveaxis((codes * scale).reshape(v.shape), -1, axis)


WIDE = False


def mx_kscale(k):
    if not WIDE:
        return np.ones(k)
    levels = np.array([10, -10, 5, -5, 0])
    a = np.random.permutation(np.resize(levels, k // 512 * 4)).reshape(k // 512, 4)
    idx = np.arange(k)
    return np.exp2(a[idx // 512, idx % 128 // 32])


BF16 = ml_dtypes.bfloat16


def bf(x):
    return np.asarray(x, np.float32).astype(BF16)


def f64(x):
    return np.asarray(x).astype(np.float64)


E2M1 = np.array([0.0, 0.5, 1.0, 1.5, 2.0, 3.0, 4.0, 6.0, -0.0, -0.5, -1.0, -1.5, -2.0, -3.0, -4.0, -6.0])


def pack_weight(w, fmt):
    k, n = w.shape
    w = f64(bf(w)).reshape(k // 32, 32, n)
    amax = np.abs(w).max(1)
    if fmt == "e4m3":
        byte = np.frexp(amax)[1] - 1 + 127 - 7
    else:
        mant, ex = np.frexp(amax / 6.0)
        byte = np.where(mant > 0.5, ex, ex - 1) + 127
    byte = np.clip(np.where(amax > 0, byte, 1), 1, 254)
    scaled = (w * np.exp2(127.0 - byte)[:, None, :]).reshape(k, n).astype(np.float32)
    by_word = np.ascontiguousarray(scaled.reshape(k // 512, 128, 4, n).transpose(0, 1, 3, 2))
    if fmt == "e4m3":
        words = by_word.astype(ml_dtypes.float8_e4m3fn).view(np.uint8)
    else:
        c = by_word.astype(ml_dtypes.float4_e2m1fn).view(np.uint8) & 0xF
        words = c[..., 0::2] | (c[..., 1::2] << 4)
    return np.ascontiguousarray(words), np.ascontiguousarray(byte.astype(np.uint8).reshape(k // 512, 16, n))


def unpack_weight(words, scales, fmt):
    g, p, n, _ = words.shape
    if fmt == "e4m3":
        vals = np.ascontiguousarray(words).view(ml_dtypes.float8_e4m3fn).astype(np.float64)
    else:
        nib = np.empty((g, p, n, 4), np.uint8)
        nib[..., 0::2] = words & 0xF
        nib[..., 1::2] = words >> 4
        vals = E2M1[nib]
    vals = vals * np.repeat(np.exp2(scales.astype(np.float64) - 127.0), 8, axis=1)[..., None]
    return vals.transpose(0, 1, 3, 2).reshape(g * 512, n)

def pack4(w):
    words, scales = pack_weight(w, "e2m1")
    return words.reshape(words.shape[0], 128, -1), scales


def unpack4(words, scales):
    return unpack_weight(words.reshape(words.shape[0], 128, -1, 2), scales, "e2m1")


B, C, E, H, HS, WS = 4, 128, 512, 16, 64, 64
N = HS * WS
EPS = 1e-5
A = 2.0 * (E / H) ** -0.5 / np.sqrt(N)


def chan_layernorm(x, g):
    mean = x.mean(axis=1, keepdims=True)
    var = x.var(axis=1, keepdims=True)
    return (x - mean) * (1.0 / np.sqrt(var + EPS)) * g


def setup_inputs():
    s = mx_kscale(E)
    h_attn = bf(np.random.standard_normal((B, E, HS, WS)) * A * s[None, :, None, None])
    xn = bf(np.random.standard_normal((B, C, HS, WS)))
    wout = np.random.standard_normal((C, E)) / (np.sqrt(E) * A) / s[None, :]
    words, scales = pack4(np.ascontiguousarray(wout.T))
    bout = bf(0.3 * np.random.standard_normal(C))
    outnorm_g = bf(1.0 + 0.1 * np.random.standard_normal((1, C, 1, 1)))
    return {"h_attn": h_attn,
            "xn": xn,
            "Wout_words": words,
            "Wout_scales": scales,
            "bout": bout,
            "outnorm_g": outnorm_g}


def reference(h_attn, xn, Wout_words, Wout_scales, bout, outnorm_g):
    a = f64(h_attn).reshape(B, E, N)
    y = (unpack4(Wout_words, Wout_scales).T @ mxq(a, 1, "e4m3")) + f64(bout)[None, :, None]
    y = y.reshape(B, C, HS, WS)
    return chan_layernorm(y, f64(outnorm_g)) + f64(xn)

@@ -1,0 +1,176 @@
+from contextlib import ExitStack
+
+import concourse.mybir as mybir
+from concourse.masks import make_identity
+
+F32 = mybir.dt.float32
+BF16 = mybir.dt.bfloat16
+I32 = mybir.dt.int32
+U32 = mybir.dt.uint32
+U8 = mybir.dt.uint8
+FP8X4 = mybir.dt.float8_e4m3fn_x4
+FP4X4 = mybir.dt.float4_e2m1fn_x4
+ACT = mybir.ActivationFunctionType
+ALU = mybir.AluOpType
+
+P = 128
+PACK = 4
+IMAGES = 4
+POSITIONS = 64 * 64
+EPS = 1e-5
+
+LOAD_POS = 2048
+QUANT_POS = 1024
+BANK_POS = 512
+BLOCK = 128
+BANKS = QUANT_POS // BANK_POS
+BLOCKS_PER_BANK = BANK_POS // BLOCK
+BLOCKS = QUANT_POS // BLOCK
+SCALAR_POS = 512
+
+FLOPS = 2 * 512 * P * IMAGES * POSITIONS
+
+
+def tile_linearattention_pb_t_kernel(tc, h_attn, xn, Wout_words, Wout_scales, bout, outnorm_g, out):
+    nc = tc.nc
+    a_view = h_attn.rearrange("b (p t) h w -> b p t (h w)", t=PACK)
+    xn_view = xn.rearrange("b c h w -> b c (h w)")
+    out_view = out.rearrange("b c h w -> b c (h w)")
+
+    with ExitStack() as ctx:
+        const = ctx.enter_context(tc.tile_pool(name="const", bufs=1))
+
+        w_words = const.tile([P, 2 * P], U8, align_bytes=64)
+        nc.sync.dma_start(out=w_words[:].bitcast(I32), in_=Wout_words[0].bitcast(I32))
+        w_plane = const.tile([P, P], U8, align_bytes=64)
+        nc.vector.memset(w_plane[:].bitcast(I32), 0)
+        for quadrant in range(4):
+            nc.sync.dma_start(
+                out=w_plane[32 * quadrant : 32 * quadrant + 4, :].bitcast(I32),
+                in_=Wout_scales[0, 4 * quadrant : 4 * quadrant + 4, :].bitcast(I32),
+            )
+
+        identity = const.tile([P, P], F32)
+        make_identity(nc, identity[:])
+        eps_col = const.tile([P, 1], F32)
+        nc.vector.memset(eps_col[:], EPS)
+
+        rows_bf = const.tile([P, P], BF16)
+        nc.vector.memset(rows_bf[:], 0.0)
+        nc.sync.dma_start(out=rows_bf[0:1, :], in_=bout.unsqueeze(0))
+        nc.sync.dma_start(out=rows_bf[1:2, :], in_=outnorm_g.rearrange("o c h w -> o (c h w)"))
+        rows_f32 = const.tile([P, P], F32)
+        nc.vector.tensor_copy(out=rows_f32[:], in_=rows_bf[:])
+        per_channel = const.tile([P, 2], F32)
+        with tc.psum_pool(name="setup_psum", bufs=1) as setup_psum:
+            cols_ps = setup_psum.tile([P, P], F32)
+            nc.tensor.transpose(cols_ps[:], rows_f32[:], identity[:])
+            nc.vector.tensor_copy(out=per_channel[:], in_=cols_ps[:, 0:2])
+        bias_col = per_channel[:, 0:1]
+        gain_col = per_channel[:, 1:2]
+
+        raw_pool = ctx.enter_context(tc.tile_pool(name="raw", bufs=3))
+        xn_pool = ctx.enter_context(tc.tile_pool(name="xn", bufs=2))
+        quant_pool = ctx.enter_context(tc.tile_pool(name="quant", bufs=2))
+        work_pool = ctx.enter_context(tc.tile_pool(name="work", bufs=2))
+        small_pool = ctx.enter_context(tc.tile_pool(name="small", bufs=3))
+        out_pool = ctx.enter_context(tc.tile_pool(name="outs", bufs=2))
+        z_psum = ctx.enter_context(tc.psum_pool(name="z_psum", bufs=2))
+        yt_psum = ctx.enter_context(tc.psum_pool(name="yt_psum", bufs=4))
+        ut_psum = ctx.enter_context(tc.psum_pool(name="ut_psum", bufs=2))
+
+        for b in range(IMAGES):
+            xn_sb = xn_pool.tile([P, POSITIONS], BF16)
+            for load in range(POSITIONS // LOAD_POS):
+                load_cols = slice(load * LOAD_POS, (load + 1) * LOAD_POS)
+                raw = raw_pool.tile([P, PACK, LOAD_POS], BF16)
+                nc.sync.dma_start(out=raw[:], in_=a_view[b, :, :, load_cols])
+                if load == 0:
+                    nc.sync.dma_start(out=xn_sb[:], in_=xn_view[b])
+                out_sb = out_pool.tile([P, LOAD_POS], F32)
+
+                for quant in range(LOAD_POS // QUANT_POS):
+                    first = quant * QUANT_POS
+
+                    grouped = quant_pool.tile([P, QUANT_POS, PACK], BF16, align_bytes=64)
+                    nc.scalar.copy(
+                        out=grouped[:, 0:SCALAR_POS, :].rearrange("p (c i) t -> p c t i", i=4),
+                        in_=raw[:, :, first : first + SCALAR_POS].rearrange("p t (c i) -> p c t i", i=4),
+                    )
+                    nc.vector.tensor_copy(
+                        out=grouped[:, SCALAR_POS:QUANT_POS, :].rearrange("p (c i) t -> p c t i", i=4),
+                        in_=raw[:, :, first + SCALAR_POS : first + QUANT_POS].rearrange("p t (c i) -> p c t i", i=4),
+                    )
+                    codes = quant_pool.tile([P, QUANT_POS], U32, align_bytes=64)
+                    scales = quant_pool.tile([P, QUANT_POS], U8, align_bytes=64)
+                    nc.vector.quantize_mx(
+                        out=codes[:].bitcast(FP8X4),
+                        scales=scales[:],
+                        in_=grouped[:].rearrange("p w t -> p (w t)"),
+                    )
+
+                    y = work_pool.tile([P, QUANT_POS], F32)
+                    for bank in range(BANKS):
+                        bank_cols = slice(bank * BANK_POS, (bank + 1) * BANK_POS)
+                        z = z_psum.tile([P, BANK_POS], F32)
+                        nc.tensor.matmul_mx(
+                            out=z[:],
+                            lhsT=w_words[:].bitcast(FP4X4),
+                            lhsT_scale=w_plane[:],
+                            rhs=codes[:, bank_cols].bitcast(FP8X4),
+                            rhs_scale=scales[:, bank_cols],
+                            start=True,
+                            stop=True,
+                        )
+                        nc.scalar.activation(out=y[:, bank_cols], in_=z[:], func=ACT.Identity, bias=bias_col)
+
+                    y_t = []
+                    stats = small_pool.tile([P, BLOCKS, 6], F32)
+                    mean_var = small_pool.tile([P, BLOCKS, 2], F32)
+                    for bank in range(BANKS):
+                        y_t_bank = yt_psum.tile([P, BLOCKS_PER_BANK, BLOCK], F32, name="y_t_bank")
+                        y_t.append(y_t_bank)
+                        for j in range(BLOCKS_PER_BANK):
+                            block = bank * BLOCKS_PER_BANK + j
+                            nc.tensor.transpose(y_t_bank[:, j, :], y[:, block * BLOCK : (block + 1) * BLOCK], identity[:])
+                        for j in range(BLOCKS_PER_BANK):
+                            block = bank * BLOCKS_PER_BANK + j
+                            nc.vector.bn_stats(out=stats[:, block, :], in_=y_t_bank[:, j, :])
+                            nc.vector.bn_aggr(out=mean_var[:, block, :], in_=stats[:, block, :])
+
+                    rstd = small_pool.tile([P, BLOCKS], F32)
+                    shift = small_pool.tile([P, BLOCKS], F32)
+                    nc.scalar.activation(out=rstd[:], in_=mean_var[:, :, 1], func=ACT.Sqrt, bias=eps_col[:])
+                    nc.vector.reciprocal(out=rstd[:], in_=rstd[:])
+                    nc.vector.scalar_tensor_tensor(
+                        out=shift[:], in0=mean_var[:, :, 0], scalar=-1.0, in1=rstd[:], op0=ALU.mult, op1=ALU.mult
+                    )
+
+                    normed = work_pool.tile([P, BLOCKS, BLOCK], F32)
+                    for bank in range(BANKS):
+                        for j in range(BLOCKS_PER_BANK):
+                            block = bank * BLOCKS_PER_BANK + j
+                            nc.scalar.activation(
+                                out=normed[:, block, :],
+                                in_=y_t[bank][:, j, :],
+                                func=ACT.Identity,
+                                scale=rstd[:, block : block + 1],
+                                bias=shift[:, block : block + 1],
+                            )
+
+                    for bank in range(BANKS):
+                        u_t = ut_psum.tile([P, BANK_POS], F32)
+                        for j in range(BLOCKS_PER_BANK):
+                            block = bank * BLOCKS_PER_BANK + j
+                            nc.tensor.transpose(u_t[:, j * BLOCK : (j + 1) * BLOCK], normed[:, block, :], identity[:])
+                        lo = first + bank * BANK_POS
+                        nc.vector.scalar_tensor_tensor(
+                            out=out_sb[:, lo : lo + BANK_POS],
+                            in0=u_t[:],
+                            scalar=gain_col,
+                            in1=xn_sb[:, load * LOAD_POS + lo : load * LOAD_POS + lo + BANK_POS],
+                            op0=ALU.mult,
+                            op1=ALU.add,
+                        )
+
+                nc.gpsimd.dma_start(out=out_view[b, :, load_cols], in_=out_sb[:])

@@ -19,14 +19,14 @@ IMAGES = 4
 POSITIONS = 64 * 64
 EPS = 1e-5
 
-LOAD_POS = 2048
-QUANT_POS = 1024
-BANK_POS = 512
+ROUND_POS = 512
 BLOCK = 128
-BANKS = QUANT_POS // BANK_POS
-BLOCKS_PER_BANK = BANK_POS // BLOCK
-BLOCKS = QUANT_POS // BLOCK
-SCALAR_POS = 512
+BLOCKS = ROUND_POS // BLOCK
+MOVE_ROUNDS = 2
+MOVE_POS = MOVE_ROUNDS * ROUND_POS
+ROUNDS_PER_IMAGE = POSITIONS // ROUND_POS
+ROUNDS = IMAGES * ROUNDS_PER_IMAGE
+LOADS_AHEAD = 2 * MOVE_ROUNDS
 
 FLOPS = 2 * 512 * P * IMAGES * POSITIONS
 
@@ -54,6 +54,8 @@ def tile_linearattention_pb_t_kernel(tc, h_attn, xn, Wout_words, Wout_scales, bo
         make_identity(nc, identity[:])
         eps_col = const.tile([P, 1], F32)
         nc.vector.memset(eps_col[:], EPS)
+        minus_average = const.tile([P, 2], F32)
+        nc.vector.memset(minus_average[:], -1.0 / P)
 
         rows_bf = const.tile([P, P], BF16)
         nc.vector.memset(rows_bf[:], 0.0)
@@ -69,108 +71,149 @@ def tile_linearattention_pb_t_kernel(tc, h_attn, xn, Wout_words, Wout_scales, bo
         bias_col = per_channel[:, 0:1]
         gain_col = per_channel[:, 1:2]
 
-        raw_pool = ctx.enter_context(tc.tile_pool(name="raw", bufs=3))
+        raw_pool = ctx.enter_context(tc.tile_pool(name="raw", bufs=4))
         xn_pool = ctx.enter_context(tc.tile_pool(name="xn", bufs=2))
-        quant_pool = ctx.enter_context(tc.tile_pool(name="quant", bufs=2))
-        work_pool = ctx.enter_context(tc.tile_pool(name="work", bufs=2))
-        small_pool = ctx.enter_context(tc.tile_pool(name="small", bufs=3))
-        out_pool = ctx.enter_context(tc.tile_pool(name="outs", bufs=2))
+        grouped_pool = ctx.enter_context(tc.tile_pool(name="grouped", bufs=3))
+        quant_pool = ctx.enter_context(tc.tile_pool(name="quant", bufs=3))
+        work_pool = ctx.enter_context(tc.tile_pool(name="work", bufs=3))
+        small_pool = ctx.enter_context(tc.tile_pool(name="small", bufs=4))
+        out_pool = ctx.enter_context(tc.tile_pool(name="outs", bufs=3))
         z_psum = ctx.enter_context(tc.psum_pool(name="z_psum", bufs=2))
-        yt_psum = ctx.enter_context(tc.psum_pool(name="yt_psum", bufs=4))
+        yt_psum = ctx.enter_context(tc.psum_pool(name="yt_psum", bufs=3))
         ut_psum = ctx.enter_context(tc.psum_pool(name="ut_psum", bufs=2))
+        mean_psum = ctx.enter_context(tc.psum_pool(name="mean_psum", bufs=1))
 
-        for b in range(IMAGES):
-            xn_sb = xn_pool.tile([P, POSITIONS], BF16)
-            for load in range(POSITIONS // LOAD_POS):
-                load_cols = slice(load * LOAD_POS, (load + 1) * LOAD_POS)
-                raw = raw_pool.tile([P, PACK, LOAD_POS], BF16)
-                nc.sync.dma_start(out=raw[:], in_=a_view[b, :, :, load_cols])
-                if load == 0:
-                    nc.sync.dma_start(out=xn_sb[:], in_=xn_view[b])
-                out_sb = out_pool.tile([P, LOAD_POS], F32)
+        raw, xn_sb, grouped, codes, scales, z, y, y_t, minus_mean_ps, minus_mean, rstd, shift, u_t, out_sb = (
+            {}, {}, {}, {}, {}, {}, {}, {}, {}, {}, {}, {}, {}, {},
+        )
 
-                for quant in range(LOAD_POS // QUANT_POS):
-                    first = quant * QUANT_POS
+        def load(r):
+            image, first = divmod(r * ROUND_POS, POSITIONS)
+            raw[r // MOVE_ROUNDS] = raw_pool.tile([P, PACK, MOVE_POS], BF16, name="raw")
+            nc.sync.dma_start(out=raw[r // MOVE_ROUNDS][:], in_=a_view[image, :, :, first : first + MOVE_POS])
+            if first == 0:
+                xn_sb[image] = xn_pool.tile([P, POSITIONS], BF16, name="xn_sb")
+                nc.sync.dma_start(out=xn_sb[image][:], in_=xn_view[image])
 
-                    grouped = quant_pool.tile([P, QUANT_POS, PACK], BF16, align_bytes=64)
-                    nc.scalar.copy(
-                        out=grouped[:, 0:SCALAR_POS, :].rearrange("p (c i) t -> p c t i", i=4),
-                        in_=raw[:, :, first : first + SCALAR_POS].rearrange("p t (c i) -> p c t i", i=4),
-                    )
-                    nc.vector.tensor_copy(
-                        out=grouped[:, SCALAR_POS:QUANT_POS, :].rearrange("p (c i) t -> p c t i", i=4),
-                        in_=raw[:, :, first + SCALAR_POS : first + QUANT_POS].rearrange("p t (c i) -> p c t i", i=4),
-                    )
-                    codes = quant_pool.tile([P, QUANT_POS], U32, align_bytes=64)
-                    scales = quant_pool.tile([P, QUANT_POS], U8, align_bytes=64)
-                    nc.vector.quantize_mx(
-                        out=codes[:].bitcast(FP8X4),
-                        scales=scales[:],
-                        in_=grouped[:].rearrange("p w t -> p (w t)"),
-                    )
+        def regroup(r):
+            first = (r % MOVE_ROUNDS) * ROUND_POS
+            grouped[r] = grouped_pool.tile([P, ROUND_POS, PACK], BF16, align_bytes=64, name="grouped")
+            nc.vector.tensor_copy(
+                out=grouped[r][:].rearrange("p (c i) t -> p c t i", i=4),
+                in_=raw[r // MOVE_ROUNDS][:, :, first : first + ROUND_POS].rearrange("p t (c i) -> p c t i", i=4),
+            )
 
-                    y = work_pool.tile([P, QUANT_POS], F32)
-                    for bank in range(BANKS):
-                        bank_cols = slice(bank * BANK_POS, (bank + 1) * BANK_POS)
-                        z = z_psum.tile([P, BANK_POS], F32)
-                        nc.tensor.matmul_mx(
-                            out=z[:],
-                            lhsT=w_words[:].bitcast(FP4X4),
-                            lhsT_scale=w_plane[:],
-                            rhs=codes[:, bank_cols].bitcast(FP8X4),
-                            rhs_scale=scales[:, bank_cols],
-                            start=True,
-                            stop=True,
-                        )
-                        nc.scalar.activation(out=y[:, bank_cols], in_=z[:], func=ACT.Identity, bias=bias_col)
+        def quantise(r):
+            codes[r] = quant_pool.tile([P, ROUND_POS], U32, align_bytes=64, name="codes")
+            scales[r] = quant_pool.tile([P, ROUND_POS], U8, align_bytes=64, name="scales")
+            nc.vector.quantize_mx(
+                out=codes[r][:].bitcast(FP8X4),
+                scales=scales[r][:],
+                in_=grouped[r][:].rearrange("p w t -> p (w t)"),
+            )
 
-                    y_t = []
-                    stats = small_pool.tile([P, BLOCKS, 6], F32)
-                    mean_var = small_pool.tile([P, BLOCKS, 2], F32)
-                    for bank in range(BANKS):
-                        y_t_bank = yt_psum.tile([P, BLOCKS_PER_BANK, BLOCK], F32, name="y_t_bank")
-                        y_t.append(y_t_bank)
-                        for j in range(BLOCKS_PER_BANK):
-                            block = bank * BLOCKS_PER_BANK + j
-                            nc.tensor.transpose(y_t_bank[:, j, :], y[:, block * BLOCK : (block + 1) * BLOCK], identity[:])
-                        for j in range(BLOCKS_PER_BANK):
-                            block = bank * BLOCKS_PER_BANK + j
-                            nc.vector.bn_stats(out=stats[:, block, :], in_=y_t_bank[:, j, :])
-                            nc.vector.bn_aggr(out=mean_var[:, block, :], in_=stats[:, block, :])
+        def multiply(r):
+            z[r] = z_psum.tile([P, ROUND_POS], F32, name="z")
+            nc.tensor.matmul_mx(
+                out=z[r][:],
+                lhsT=w_words[:].bitcast(FP4X4),
+                lhsT_scale=w_plane[:],
+                rhs=codes[r][:].bitcast(FP8X4),
+                rhs_scale=scales[r][:],
+                start=True,
+                stop=True,
+            )
 
-                    rstd = small_pool.tile([P, BLOCKS], F32)
-                    shift = small_pool.tile([P, BLOCKS], F32)
-                    nc.scalar.activation(out=rstd[:], in_=mean_var[:, :, 1], func=ACT.Sqrt, bias=eps_col[:])
-                    nc.vector.reciprocal(out=rstd[:], in_=rstd[:])
-                    nc.vector.scalar_tensor_tensor(
-                        out=shift[:], in0=mean_var[:, :, 0], scalar=-1.0, in1=rstd[:], op0=ALU.mult, op1=ALU.mult
-                    )
+        def add_bias(r):
+            y[r] = work_pool.tile([P, ROUND_POS], F32, name="y")
+            nc.scalar.activation(out=y[r][:], in_=z[r][:], func=ACT.Identity, bias=bias_col)
 
-                    normed = work_pool.tile([P, BLOCKS, BLOCK], F32)
-                    for bank in range(BANKS):
-                        for j in range(BLOCKS_PER_BANK):
-                            block = bank * BLOCKS_PER_BANK + j
-                            nc.scalar.activation(
-                                out=normed[:, block, :],
-                                in_=y_t[bank][:, j, :],
-                                func=ACT.Identity,
-                                scale=rstd[:, block : block + 1],
-                                bias=shift[:, block : block + 1],
-                            )
+        def turn(r):
+            minus_mean_ps[r] = mean_psum.tile([P, BLOCKS, 2], F32, name="minus_mean_ps")
+            for block in range(BLOCKS):
+                nc.tensor.matmul(
+                    out=minus_mean_ps[r][:, block, :],
+                    lhsT=y[r][:, block * BLOCK : (block + 1) * BLOCK],
+                    rhs=minus_average[:],
+                    start=True,
+                    stop=True,
+                )
+            y_t[r] = yt_psum.tile([P, BLOCKS, BLOCK], F32, name="y_t")
+            for block in range(BLOCKS):
+                nc.tensor.transpose(y_t[r][:, block, :], y[r][:, block * BLOCK : (block + 1) * BLOCK], identity[:])
 
-                    for bank in range(BANKS):
-                        u_t = ut_psum.tile([P, BANK_POS], F32)
-                        for j in range(BLOCKS_PER_BANK):
-                            block = bank * BLOCKS_PER_BANK + j
-                            nc.tensor.transpose(u_t[:, j * BLOCK : (j + 1) * BLOCK], normed[:, block, :], identity[:])
-                        lo = first + bank * BANK_POS
-                        nc.vector.scalar_tensor_tensor(
-                            out=out_sb[:, lo : lo + BANK_POS],
-                            in0=u_t[:],
-                            scalar=gain_col,
-                            in1=xn_sb[:, load * LOAD_POS + lo : load * LOAD_POS + lo + BANK_POS],
-                            op0=ALU.mult,
-                            op1=ALU.add,
-                        )
+        def statistics(r):
+            minus_mean[r] = small_pool.tile([P, BLOCKS], F32, name="minus_mean")
+            nc.scalar.copy(out=minus_mean[r][:], in_=minus_mean_ps[r][:, :, 0])
+            squares = work_pool.tile([P, BLOCKS, BLOCK], F32, name="squares")
+            sum_squares = small_pool.tile([P, BLOCKS], F32, name="sum_squares")
+            for block in range(BLOCKS):
+                nc.scalar.activation(
+                    out=squares[:, block, :],
+                    in_=y_t[r][:, block, :],
+                    func=ACT.Square,
+                    bias=minus_mean[r][:, block : block + 1],
+                    accum_out=sum_squares[:, block : block + 1],
+                )
+            std = small_pool.tile([P, BLOCKS], F32, name="std")
+            nc.scalar.activation(out=std[:], in_=sum_squares[:], func=ACT.Sqrt, scale=1.0 / P, bias=eps_col[:])
+            rstd[r] = small_pool.tile([P, BLOCKS], F32, name="rstd")
+            nc.vector.reciprocal(out=rstd[r][:], in_=std[:])
+            shift[r] = small_pool.tile([P, BLOCKS], F32, name="shift")
+            nc.vector.tensor_tensor(out=shift[r][:], in0=minus_mean[r][:], in1=rstd[r][:], op=ALU.mult)
 
-                nc.gpsimd.dma_start(out=out_view[b, :, load_cols], in_=out_sb[:])
+        def normalise(r):
+            normed = work_pool.tile([P, BLOCKS, BLOCK], F32, name="normed")
+            for block in range(BLOCKS):
+                nc.scalar.activation(
+                    out=normed[:, block, :],
+                    in_=y_t[r][:, block, :],
+                    func=ACT.Identity,
+                    scale=rstd[r][:, block : block + 1],
+                    bias=shift[r][:, block : block + 1],
+                )
+            u_t[r] = ut_psum.tile([P, ROUND_POS], F32, name="u_t")
+            for block in range(BLOCKS):
+                nc.tensor.transpose(u_t[r][:, block * BLOCK : (block + 1) * BLOCK], normed[:, block, :], identity[:])
+
+        def finish(r):
+            image, first = divmod(r * ROUND_POS, POSITIONS)
+            part = r % MOVE_ROUNDS
+            if part == 0:
+                out_sb[r // MOVE_ROUNDS] = out_pool.tile([P, MOVE_POS], F32, name="out_sb")
+            nc.vector.scalar_tensor_tensor(
+                out=out_sb[r // MOVE_ROUNDS][:, part * ROUND_POS : (part + 1) * ROUND_POS],
+                in0=u_t[r][:],
+                scalar=gain_col,
+                in1=xn_sb[image][:, first : first + ROUND_POS],
+                op0=ALU.mult,
+                op1=ALU.add,
+            )
+            if part == MOVE_ROUNDS - 1:
+                last = first + ROUND_POS
+                nc.sync.dma_start(out=out_view[image, :, last - MOVE_POS : last], in_=out_sb[r // MOVE_ROUNDS][:])
+
+        def is_round(r):
+            return 0 <= r < ROUNDS
+
+        with tc.manual_schedule():
+            for now in range(-LOADS_AHEAD, ROUNDS + 5):
+                ahead = now + LOADS_AHEAD
+                if is_round(ahead) and ahead % MOVE_ROUNDS == 0:
+                    load(ahead)
+                if is_round(now - 3):
+                    turn(now - 3)
+                if is_round(now - 2):
+                    multiply(now - 2)
+                if is_round(now - 4):
+                    normalise(now - 4)
+                if is_round(now - 5):
+                    finish(now - 5)
+                if is_round(now - 1):
+                    quantise(now - 1)
+                if is_round(now):
+                    regroup(now)
+                if is_round(now - 3):
+                    statistics(now - 3)
+                if is_round(now - 2):
+                    add_bias(now - 2)

@@ -19,14 +19,17 @@ IMAGES = 4
 POSITIONS = 64 * 64
 EPS = 1e-5
 
-ROUND_POS = 512
+LOAD_POS = 2048
+QUANT_POS = 1024
+BANK_POS = 512
 BLOCK = 128
-BLOCKS = ROUND_POS // BLOCK
-MOVE_ROUNDS = 2
-MOVE_POS = MOVE_ROUNDS * ROUND_POS
-ROUNDS_PER_IMAGE = POSITIONS // ROUND_POS
-ROUNDS = IMAGES * ROUNDS_PER_IMAGE
-LOADS_AHEAD = 2 * MOVE_ROUNDS
+BANKS = QUANT_POS // BANK_POS
+BLOCKS_PER_BANK = BANK_POS // BLOCK
+BLOCKS = QUANT_POS // BLOCK
+SCALAR_POS = 320
+VECTOR_POS = 192
+GPSIMD_POS = QUANT_POS - SCALAR_POS - VECTOR_POS
+GPSIMD_PIECE = 128
 
 FLOPS = 2 * 512 * P * IMAGES * POSITIONS
 
@@ -54,8 +57,6 @@ def tile_linearattention_pb_t_kernel(tc, h_attn, xn, Wout_words, Wout_scales, bo
         make_identity(nc, identity[:])
         eps_col = const.tile([P, 1], F32)
         nc.vector.memset(eps_col[:], EPS)
-        minus_average = const.tile([P, 2], F32)
-        nc.vector.memset(minus_average[:], -1.0 / P)
 
         rows_bf = const.tile([P, P], BF16)
         nc.vector.memset(rows_bf[:], 0.0)
@@ -71,149 +72,118 @@ def tile_linearattention_pb_t_kernel(tc, h_attn, xn, Wout_words, Wout_scales, bo
         bias_col = per_channel[:, 0:1]
         gain_col = per_channel[:, 1:2]
 
-        raw_pool = ctx.enter_context(tc.tile_pool(name="raw", bufs=4))
+        raw_pool = ctx.enter_context(tc.tile_pool(name="raw", bufs=3))
         xn_pool = ctx.enter_context(tc.tile_pool(name="xn", bufs=2))
-        grouped_pool = ctx.enter_context(tc.tile_pool(name="grouped", bufs=3))
-        quant_pool = ctx.enter_context(tc.tile_pool(name="quant", bufs=3))
-        work_pool = ctx.enter_context(tc.tile_pool(name="work", bufs=3))
-        small_pool = ctx.enter_context(tc.tile_pool(name="small", bufs=4))
-        out_pool = ctx.enter_context(tc.tile_pool(name="outs", bufs=3))
+        quant_pool = ctx.enter_context(tc.tile_pool(name="quant", bufs=2))
+        work_pool = ctx.enter_context(tc.tile_pool(name="work", bufs=2))
+        small_pool = ctx.enter_context(tc.tile_pool(name="small", bufs=3))
+        out_pool = ctx.enter_context(tc.tile_pool(name="outs", bufs=2))
         z_psum = ctx.enter_context(tc.psum_pool(name="z_psum", bufs=2))
-        yt_psum = ctx.enter_context(tc.psum_pool(name="yt_psum", bufs=3))
+        yt_psum = ctx.enter_context(tc.psum_pool(name="yt_psum", bufs=4))
         ut_psum = ctx.enter_context(tc.psum_pool(name="ut_psum", bufs=2))
-        mean_psum = ctx.enter_context(tc.psum_pool(name="mean_psum", bufs=1))
 
-        raw, xn_sb, grouped, codes, scales, z, y, y_t, minus_mean_ps, minus_mean, rstd, shift, u_t, out_sb = (
-            {}, {}, {}, {}, {}, {}, {}, {}, {}, {}, {}, {}, {}, {},
-        )
+        for b in range(IMAGES):
+            xn_sb = xn_pool.tile([P, POSITIONS], BF16)
+            for load in range(POSITIONS // LOAD_POS):
+                load_cols = slice(load * LOAD_POS, (load + 1) * LOAD_POS)
+                raw = raw_pool.tile([P, PACK, LOAD_POS], BF16)
+                nc.sync.dma_start(out=raw[:], in_=a_view[b, :, :, load_cols])
+                if load == 0:
+                    nc.sync.dma_start(out=xn_sb[:], in_=xn_view[b])
+                out_sb = out_pool.tile([P, LOAD_POS], F32)
 
-        def load(r):
-            image, first = divmod(r * ROUND_POS, POSITIONS)
-            raw[r // MOVE_ROUNDS] = raw_pool.tile([P, PACK, MOVE_POS], BF16, name="raw")
-            nc.sync.dma_start(out=raw[r // MOVE_ROUNDS][:], in_=a_view[image, :, :, first : first + MOVE_POS])
-            if first == 0:
-                xn_sb[image] = xn_pool.tile([P, POSITIONS], BF16, name="xn_sb")
-                nc.sync.dma_start(out=xn_sb[image][:], in_=xn_view[image])
+                for quant in range(LOAD_POS // QUANT_POS):
+                    first = quant * QUANT_POS
 
-        def regroup(r):
-            first = (r % MOVE_ROUNDS) * ROUND_POS
-            grouped[r] = grouped_pool.tile([P, ROUND_POS, PACK], BF16, align_bytes=64, name="grouped")
-            nc.vector.tensor_copy(
-                out=grouped[r][:].rearrange("p (c i) t -> p c t i", i=4),
-                in_=raw[r // MOVE_ROUNDS][:, :, first : first + ROUND_POS].rearrange("p t (c i) -> p c t i", i=4),
-            )
+                    grouped = quant_pool.tile([P, QUANT_POS, PACK], BF16, align_bytes=64)
+                    nc.scalar.copy(
+                        out=grouped[:, 0:SCALAR_POS, :].rearrange("p (c i) t -> p c t i", i=4),
+                        in_=raw[:, :, first : first + SCALAR_POS].rearrange("p t (c i) -> p c t i", i=4),
+                    )
+                    vector_end = SCALAR_POS + VECTOR_POS
+                    nc.vector.tensor_copy(
+                        out=grouped[:, SCALAR_POS:vector_end, :].rearrange("p (c i) t -> p c t i", i=4),
+                        in_=raw[:, :, first + SCALAR_POS : first + vector_end].rearrange("p t (c i) -> p c t i", i=4),
+                    )
+                    for lo in range(vector_end, QUANT_POS, GPSIMD_PIECE):
+                        nc.gpsimd.tensor_scalar(
+                            out=grouped[:, lo : lo + GPSIMD_PIECE, :].rearrange("p (c i) t -> p c t i", i=4),
+                            in0=raw[:, :, first + lo : first + lo + GPSIMD_PIECE].rearrange("p t (c i) -> p c t i", i=4),
+                            scalar1=1.0,
+                            scalar2=0.0,
+                            op0=ALU.mult,
+                            op1=ALU.add,
+                        )
+                    codes = quant_pool.tile([P, QUANT_POS], U32, align_bytes=64)
+                    scales = quant_pool.tile([P, QUANT_POS], U8, align_bytes=64)
+                    nc.vector.quantize_mx(
+                        out=codes[:].bitcast(FP8X4),
+                        scales=scales[:],
+                        in_=grouped[:].rearrange("p w t -> p (w t)"),
+                    )
 
-        def quantise(r):
-            codes[r] = quant_pool.tile([P, ROUND_POS], U32, align_bytes=64, name="codes")
-            scales[r] = quant_pool.tile([P, ROUND_POS], U8, align_bytes=64, name="scales")
-            nc.vector.quantize_mx(
-                out=codes[r][:].bitcast(FP8X4),
-                scales=scales[r][:],
-                in_=grouped[r][:].rearrange("p w t -> p (w t)"),
-            )
+                    y = work_pool.tile([P, QUANT_POS], F32)
+                    for bank in range(BANKS):
+                        bank_cols = slice(bank * BANK_POS, (bank + 1) * BANK_POS)
+                        z = z_psum.tile([P, BANK_POS], F32)
+                        nc.tensor.matmul_mx(
+                            out=z[:],
+                            lhsT=w_words[:].bitcast(FP4X4),
+                            lhsT_scale=w_plane[:],
+                            rhs=codes[:, bank_cols].bitcast(FP8X4),
+                            rhs_scale=scales[:, bank_cols],
+                            start=True,
+                            stop=True,
+                        )
+                        nc.scalar.activation(out=y[:, bank_cols], in_=z[:], func=ACT.Identity, bias=bias_col)
 
-        def multiply(r):
-            z[r] = z_psum.tile([P, ROUND_POS], F32, name="z")
-            nc.tensor.matmul_mx(
-                out=z[r][:],
-                lhsT=w_words[:].bitcast(FP4X4),
-                lhsT_scale=w_plane[:],
-                rhs=codes[r][:].bitcast(FP8X4),
-                rhs_scale=scales[r][:],
-                start=True,
-                stop=True,
-            )
+                    y_t = []
+                    stats = small_pool.tile([P, BLOCKS, 6], F32)
+                    mean_var = small_pool.tile([P, BLOCKS, 2], F32)
+                    for bank in range(BANKS):
+                        y_t_bank = yt_psum.tile([P, BLOCKS_PER_BANK, BLOCK], F32, name="y_t_bank")
+                        y_t.append(y_t_bank)
+                        for j in range(BLOCKS_PER_BANK):
+                            block = bank * BLOCKS_PER_BANK + j
+                            nc.tensor.transpose(y_t_bank[:, j, :], y[:, block * BLOCK : (block + 1) * BLOCK], identity[:])
+                        for j in range(BLOCKS_PER_BANK):
+                            block = bank * BLOCKS_PER_BANK + j
+                            nc.vector.bn_stats(out=stats[:, block, :], in_=y_t_bank[:, j, :])
+                            nc.vector.bn_aggr(out=mean_var[:, block, :], in_=stats[:, block, :])
 
-        def add_bias(r):
-            y[r] = work_pool.tile([P, ROUND_POS], F32, name="y")
-            nc.scalar.activation(out=y[r][:], in_=z[r][:], func=ACT.Identity, bias=bias_col)
+                    rstd = small_pool.tile([P, BLOCKS], F32)
+                    shift = small_pool.tile([P, BLOCKS], F32)
+                    nc.scalar.activation(out=rstd[:], in_=mean_var[:, :, 1], func=ACT.Sqrt, bias=eps_col[:])
+                    nc.vector.reciprocal(out=rstd[:], in_=rstd[:])
+                    nc.vector.scalar_tensor_tensor(
+                        out=shift[:], in0=mean_var[:, :, 0], scalar=-1.0, in1=rstd[:], op0=ALU.mult, op1=ALU.mult
+                    )
 
-        def turn(r):
-            minus_mean_ps[r] = mean_psum.tile([P, BLOCKS, 2], F32, name="minus_mean_ps")
-            for block in range(BLOCKS):
-                nc.tensor.matmul(
-                    out=minus_mean_ps[r][:, block, :],
-                    lhsT=y[r][:, block * BLOCK : (block + 1) * BLOCK],
-                    rhs=minus_average[:],
-                    start=True,
-                    stop=True,
-                )
-            y_t[r] = yt_psum.tile([P, BLOCKS, BLOCK], F32, name="y_t")
-            for block in range(BLOCKS):
-                nc.tensor.transpose(y_t[r][:, block, :], y[r][:, block * BLOCK : (block + 1) * BLOCK], identity[:])
+                    normed = work_pool.tile([P, BLOCKS, BLOCK], F32)
+                    for bank in range(BANKS):
+                        for j in range(BLOCKS_PER_BANK):
+                            block = bank * BLOCKS_PER_BANK + j
+                            nc.scalar.activation(
+                                out=normed[:, block, :],
+                                in_=y_t[bank][:, j, :],
+                                func=ACT.Identity,
+                                scale=rstd[:, block : block + 1],
+                                bias=shift[:, block : block + 1],
+                            )
 
-        def statistics(r):
-            minus_mean[r] = small_pool.tile([P, BLOCKS], F32, name="minus_mean")
-            nc.scalar.copy(out=minus_mean[r][:], in_=minus_mean_ps[r][:, :, 0])
-            squares = work_pool.tile([P, BLOCKS, BLOCK], F32, name="squares")
-            sum_squares = small_pool.tile([P, BLOCKS], F32, name="sum_squares")
-            for block in range(BLOCKS):
-                nc.scalar.activation(
-                    out=squares[:, block, :],
-                    in_=y_t[r][:, block, :],
-                    func=ACT.Square,
-                    bias=minus_mean[r][:, block : block + 1],
-                    accum_out=sum_squares[:, block : block + 1],
-                )
-            std = small_pool.tile([P, BLOCKS], F32, name="std")
-            nc.scalar.activation(out=std[:], in_=sum_squares[:], func=ACT.Sqrt, scale=1.0 / P, bias=eps_col[:])
-            rstd[r] = small_pool.tile([P, BLOCKS], F32, name="rstd")
-            nc.vector.reciprocal(out=rstd[r][:], in_=std[:])
-            shift[r] = small_pool.tile([P, BLOCKS], F32, name="shift")
-            nc.vector.tensor_tensor(out=shift[r][:], in0=minus_mean[r][:], in1=rstd[r][:], op=ALU.mult)
+                    for bank in range(BANKS):
+                        u_t = ut_psum.tile([P, BANK_POS], F32)
+                        for j in range(BLOCKS_PER_BANK):
+                            block = bank * BLOCKS_PER_BANK + j
+                            nc.tensor.transpose(u_t[:, j * BLOCK : (j + 1) * BLOCK], normed[:, block, :], identity[:])
+                        lo = first + bank * BANK_POS
+                        nc.vector.scalar_tensor_tensor(
+                            out=out_sb[:, lo : lo + BANK_POS],
+                            in0=u_t[:],
+                            scalar=gain_col,
+                            in1=xn_sb[:, load * LOAD_POS + lo : load * LOAD_POS + lo + BANK_POS],
+                            op0=ALU.mult,
+                            op1=ALU.add,
+                        )
 
-        def normalise(r):
-            normed = work_pool.tile([P, BLOCKS, BLOCK], F32, name="normed")
-            for block in range(BLOCKS):
-                nc.scalar.activation(
-                    out=normed[:, block, :],
-                    in_=y_t[r][:, block, :],
-                    func=ACT.Identity,
-                    scale=rstd[r][:, block : block + 1],
-                    bias=shift[r][:, block : block + 1],
-                )
-            u_t[r] = ut_psum.tile([P, ROUND_POS], F32, name="u_t")
-            for block in range(BLOCKS):
-                nc.tensor.transpose(u_t[r][:, block * BLOCK : (block + 1) * BLOCK], normed[:, block, :], identity[:])
-
-        def finish(r):
-            image, first = divmod(r * ROUND_POS, POSITIONS)
-            part = r % MOVE_ROUNDS
-            if part == 0:
-                out_sb[r // MOVE_ROUNDS] = out_pool.tile([P, MOVE_POS], F32, name="out_sb")
-            nc.vector.scalar_tensor_tensor(
-                out=out_sb[r // MOVE_ROUNDS][:, part * ROUND_POS : (part + 1) * ROUND_POS],
-                in0=u_t[r][:],
-                scalar=gain_col,
-                in1=xn_sb[image][:, first : first + ROUND_POS],
-                op0=ALU.mult,
-                op1=ALU.add,
-            )
-            if part == MOVE_ROUNDS - 1:
-                last = first + ROUND_POS
-                nc.sync.dma_start(out=out_view[image, :, last - MOVE_POS : last], in_=out_sb[r // MOVE_ROUNDS][:])
-
-        def is_round(r):
-            return 0 <= r < ROUNDS
-
-        with tc.manual_schedule():
-            for now in range(-LOADS_AHEAD, ROUNDS + 5):
-                ahead = now + LOADS_AHEAD
-                if is_round(ahead) and ahead % MOVE_ROUNDS == 0:
-                    load(ahead)
-                if is_round(now - 3):
-                    turn(now - 3)
-                if is_round(now - 2):
-                    multiply(now - 2)
-                if is_round(now - 4):
-                    normalise(now - 4)
-                if is_round(now - 5):
-                    finish(now - 5)
-                if is_round(now - 1):
-                    quantise(now - 1)
-                if is_round(now):
-                    regroup(now)
-                if is_round(now - 3):
-                    statistics(now - 3)
-                if is_round(now - 2):
-                    add_bias(now - 2)
+                nc.sync.dma_start(out=out_view[b, :, load_cols], in_=out_sb[:])

@@ -19,17 +19,18 @@ IMAGES = 4
 POSITIONS = 64 * 64
 EPS = 1e-5
 
-LOAD_POS = 2048
-QUANT_POS = 1024
-BANK_POS = 512
+BANK = 512
 BLOCK = 128
-BANKS = QUANT_POS // BANK_POS
-BLOCKS_PER_BANK = BANK_POS // BLOCK
-BLOCKS = QUANT_POS // BLOCK
-SCALAR_POS = 320
-VECTOR_POS = 192
-GPSIMD_POS = QUANT_POS - SCALAR_POS - VECTOR_POS
-GPSIMD_PIECE = 128
+BLOCKS = BANK // BLOCK
+BANKS_PER_IMAGE = POSITIONS // BANK
+N_BANKS = IMAGES * BANKS_PER_IMAGE
+LOAD_BANKS = 4
+N_LOADS = N_BANKS // LOAD_BANKS
+RAW_BUFS = 3
+STORE_BANKS = 2
+GROUPED_BUFS = 2
+SCALAR_POS = 224
+GPSIMD_POS = BANK - SCALAR_POS
 
 FLOPS = 2 * 512 * P * IMAGES * POSITIONS
 
@@ -42,6 +43,35 @@ def tile_linearattention_pb_t_kernel(tc, h_attn, xn, Wout_words, Wout_scales, bo
 
     with ExitStack() as ctx:
         const = ctx.enter_context(tc.tile_pool(name="const", bufs=1))
+        head_pool = ctx.enter_context(tc.tile_pool(name="head", bufs=LOAD_BANKS))
+        raw_pool = ctx.enter_context(tc.tile_pool(name="raw", bufs=RAW_BUFS))
+        xn_pool = ctx.enter_context(tc.tile_pool(name="xn", bufs=2))
+
+        raw_of_bank = {}
+
+        def load_head(j):
+            t = head_pool.tile([P, PACK, BANK], BF16, name="head")
+            nc.sync.dma_start(out=t[:], in_=a_view[0, :, :, j * BANK : (j + 1) * BANK])
+            raw_of_bank[j] = t[:]
+
+        def load_raw(k):
+            t = raw_pool.tile([P, PACK, LOAD_BANKS * BANK], BF16, name="raw")
+            first = k * LOAD_BANKS
+            b = first // BANKS_PER_IMAGE
+            lo = (first % BANKS_PER_IMAGE) * BANK
+            nc.sync.dma_start(out=t[:], in_=a_view[b, :, :, lo : lo + LOAD_BANKS * BANK])
+            for i in range(LOAD_BANKS):
+                raw_of_bank[first + i] = t[:, :, i * BANK : (i + 1) * BANK]
+
+        xn_of_image = {}
+
+        def load_xn(b):
+            t = xn_pool.tile([P, POSITIONS], BF16, name="xn_sb")
+            nc.sync.dma_start(out=t[:], in_=xn_view[b])
+            xn_of_image[b] = t
+
+        load_head(0)
+        load_head(1)
 
         w_words = const.tile([P, 2 * P], U8, align_bytes=64)
         nc.sync.dma_start(out=w_words[:].bitcast(I32), in_=Wout_words[0].bitcast(I32))
@@ -57,11 +87,20 @@ def tile_linearattention_pb_t_kernel(tc, h_attn, xn, Wout_words, Wout_scales, bo
         make_identity(nc, identity[:])
         eps_col = const.tile([P, 1], F32)
         nc.vector.memset(eps_col[:], EPS)
+        warm = const.tile([P, 1], F32)
+        nc.scalar.activation(out=warm[:], in_=eps_col[:], func=ACT.Abs_reciprocal_sqrt)
 
         rows_bf = const.tile([P, P], BF16)
         nc.vector.memset(rows_bf[:], 0.0)
         nc.sync.dma_start(out=rows_bf[0:1, :], in_=bout.unsqueeze(0))
         nc.sync.dma_start(out=rows_bf[1:2, :], in_=outnorm_g.rearrange("o c h w -> o (c h w)"))
+        load_head(2)
+        load_head(3)
+        load_raw(1)
+        load_xn(0)
+        load_raw(2)
+        load_raw(3)
+        load_xn(1)
         rows_f32 = const.tile([P, P], F32)
         nc.vector.tensor_copy(out=rows_f32[:], in_=rows_bf[:])
         per_channel = const.tile([P, 2], F32)
@@ -72,118 +111,166 @@ def tile_linearattention_pb_t_kernel(tc, h_attn, xn, Wout_words, Wout_scales, bo
         bias_col = per_channel[:, 0:1]
         gain_col = per_channel[:, 1:2]
 
-        raw_pool = ctx.enter_context(tc.tile_pool(name="raw", bufs=3))
-        xn_pool = ctx.enter_context(tc.tile_pool(name="xn", bufs=2))
-        quant_pool = ctx.enter_context(tc.tile_pool(name="quant", bufs=2))
-        work_pool = ctx.enter_context(tc.tile_pool(name="work", bufs=2))
-        small_pool = ctx.enter_context(tc.tile_pool(name="small", bufs=3))
-        out_pool = ctx.enter_context(tc.tile_pool(name="outs", bufs=2))
+        grouped_pool = ctx.enter_context(tc.tile_pool(name="grouped", bufs=GROUPED_BUFS))
+        quant_pool = ctx.enter_context(tc.tile_pool(name="quant", bufs=3))
+        work_pool = ctx.enter_context(tc.tile_pool(name="work", bufs=3))
+        small_pool = ctx.enter_context(tc.tile_pool(name="small", bufs=6))
+        out_pool = ctx.enter_context(tc.tile_pool(name="outs", bufs=3))
         z_psum = ctx.enter_context(tc.psum_pool(name="z_psum", bufs=2))
         yt_psum = ctx.enter_context(tc.psum_pool(name="yt_psum", bufs=4))
         ut_psum = ctx.enter_context(tc.psum_pool(name="ut_psum", bufs=2))
 
-        for b in range(IMAGES):
-            xn_sb = xn_pool.tile([P, POSITIONS], BF16)
-            for load in range(POSITIONS // LOAD_POS):
-                load_cols = slice(load * LOAD_POS, (load + 1) * LOAD_POS)
-                raw = raw_pool.tile([P, PACK, LOAD_POS], BF16)
-                nc.sync.dma_start(out=raw[:], in_=a_view[b, :, :, load_cols])
-                if load == 0:
-                    nc.sync.dma_start(out=xn_sb[:], in_=xn_view[b])
-                out_sb = out_pool.tile([P, LOAD_POS], F32)
+        grouped, codes, scales, z, y, y_t = {}, {}, {}, {}, {}, {}
+        mean_var, rstd, shift, normed, u_t, out_sb = {}, {}, {}, {}, {}, {}
 
-                for quant in range(LOAD_POS // QUANT_POS):
-                    first = quant * QUANT_POS
+        def ok(j):
+            return 0 <= j < N_BANKS
 
-                    grouped = quant_pool.tile([P, QUANT_POS, PACK], BF16, align_bytes=64)
-                    nc.scalar.copy(
-                        out=grouped[:, 0:SCALAR_POS, :].rearrange("p (c i) t -> p c t i", i=4),
-                        in_=raw[:, :, first : first + SCALAR_POS].rearrange("p t (c i) -> p c t i", i=4),
-                    )
-                    vector_end = SCALAR_POS + VECTOR_POS
-                    nc.vector.tensor_copy(
-                        out=grouped[:, SCALAR_POS:vector_end, :].rearrange("p (c i) t -> p c t i", i=4),
-                        in_=raw[:, :, first + SCALAR_POS : first + vector_end].rearrange("p t (c i) -> p c t i", i=4),
-                    )
-                    for lo in range(vector_end, QUANT_POS, GPSIMD_PIECE):
-                        nc.gpsimd.tensor_scalar(
-                            out=grouped[:, lo : lo + GPSIMD_PIECE, :].rearrange("p (c i) t -> p c t i", i=4),
-                            in0=raw[:, :, first + lo : first + lo + GPSIMD_PIECE].rearrange("p t (c i) -> p c t i", i=4),
-                            scalar1=1.0,
-                            scalar2=0.0,
-                            op0=ALU.mult,
-                            op1=ALU.add,
-                        )
-                    codes = quant_pool.tile([P, QUANT_POS], U32, align_bytes=64)
-                    scales = quant_pool.tile([P, QUANT_POS], U8, align_bytes=64)
-                    nc.vector.quantize_mx(
-                        out=codes[:].bitcast(FP8X4),
-                        scales=scales[:],
-                        in_=grouped[:].rearrange("p w t -> p (w t)"),
-                    )
+        def runs_of_4(dst, src):
+            return (
+                dst.rearrange("p (c i) t -> p c t i", i=4),
+                src.rearrange("p t (c i) -> p c t i", i=4),
+            )
 
-                    y = work_pool.tile([P, QUANT_POS], F32)
-                    for bank in range(BANKS):
-                        bank_cols = slice(bank * BANK_POS, (bank + 1) * BANK_POS)
-                        z = z_psum.tile([P, BANK_POS], F32)
-                        nc.tensor.matmul_mx(
-                            out=z[:],
-                            lhsT=w_words[:].bitcast(FP4X4),
-                            lhsT_scale=w_plane[:],
-                            rhs=codes[:, bank_cols].bitcast(FP8X4),
-                            rhs_scale=scales[:, bank_cols],
-                            start=True,
-                            stop=True,
-                        )
-                        nc.scalar.activation(out=y[:, bank_cols], in_=z[:], func=ACT.Identity, bias=bias_col)
+        def regroup_scalar(j):
+            grouped[j] = grouped_pool.tile([P, BANK, PACK], BF16, align_bytes=64, name="grouped")
+            dst, src = runs_of_4(grouped[j][:, 0:SCALAR_POS, :], raw_of_bank[j][:, :, 0:SCALAR_POS])
+            nc.scalar.copy(out=dst, in_=src)
 
-                    y_t = []
-                    stats = small_pool.tile([P, BLOCKS, 6], F32)
-                    mean_var = small_pool.tile([P, BLOCKS, 2], F32)
-                    for bank in range(BANKS):
-                        y_t_bank = yt_psum.tile([P, BLOCKS_PER_BANK, BLOCK], F32, name="y_t_bank")
-                        y_t.append(y_t_bank)
-                        for j in range(BLOCKS_PER_BANK):
-                            block = bank * BLOCKS_PER_BANK + j
-                            nc.tensor.transpose(y_t_bank[:, j, :], y[:, block * BLOCK : (block + 1) * BLOCK], identity[:])
-                        for j in range(BLOCKS_PER_BANK):
-                            block = bank * BLOCKS_PER_BANK + j
-                            nc.vector.bn_stats(out=stats[:, block, :], in_=y_t_bank[:, j, :])
-                            nc.vector.bn_aggr(out=mean_var[:, block, :], in_=stats[:, block, :])
+        def regroup_gpsimd(j):
+            hi = SCALAR_POS + GPSIMD_POS
+            nc.gpsimd.tensor_scalar(
+                out=grouped[j][:, SCALAR_POS:hi, :],
+                in0=raw_of_bank[j][:, :, SCALAR_POS:hi].rearrange("p t w -> p w t"),
+                scalar1=1.0,
+                scalar2=0.0,
+                op0=ALU.mult,
+                op1=ALU.add,
+            )
 
-                    rstd = small_pool.tile([P, BLOCKS], F32)
-                    shift = small_pool.tile([P, BLOCKS], F32)
-                    nc.scalar.activation(out=rstd[:], in_=mean_var[:, :, 1], func=ACT.Sqrt, bias=eps_col[:])
-                    nc.vector.reciprocal(out=rstd[:], in_=rstd[:])
-                    nc.vector.scalar_tensor_tensor(
-                        out=shift[:], in0=mean_var[:, :, 0], scalar=-1.0, in1=rstd[:], op0=ALU.mult, op1=ALU.mult
-                    )
+        def quantise(j):
+            codes[j] = quant_pool.tile([P, BANK], U32, align_bytes=64, name="codes")
+            scales[j] = quant_pool.tile([P, BANK], U8, align_bytes=64, name="scales")
+            nc.vector.quantize_mx(
+                out=codes[j][:].bitcast(FP8X4),
+                scales=scales[j][:],
+                in_=grouped[j][:].rearrange("p w t -> p (w t)"),
+            )
 
-                    normed = work_pool.tile([P, BLOCKS, BLOCK], F32)
-                    for bank in range(BANKS):
-                        for j in range(BLOCKS_PER_BANK):
-                            block = bank * BLOCKS_PER_BANK + j
-                            nc.scalar.activation(
-                                out=normed[:, block, :],
-                                in_=y_t[bank][:, j, :],
-                                func=ACT.Identity,
-                                scale=rstd[:, block : block + 1],
-                                bias=shift[:, block : block + 1],
-                            )
+        def project(j):
+            z[j] = z_psum.tile([P, BANK], F32, name="z")
+            nc.tensor.matmul_mx(
+                out=z[j][:],
+                lhsT=w_words[:].bitcast(FP4X4),
+                lhsT_scale=w_plane[:],
+                rhs=codes[j][:].bitcast(FP8X4),
+                rhs_scale=scales[j][:],
+                start=True,
+                stop=True,
+            )
 
-                    for bank in range(BANKS):
-                        u_t = ut_psum.tile([P, BANK_POS], F32)
-                        for j in range(BLOCKS_PER_BANK):
-                            block = bank * BLOCKS_PER_BANK + j
-                            nc.tensor.transpose(u_t[:, j * BLOCK : (j + 1) * BLOCK], normed[:, block, :], identity[:])
-                        lo = first + bank * BANK_POS
-                        nc.vector.scalar_tensor_tensor(
-                            out=out_sb[:, lo : lo + BANK_POS],
-                            in0=u_t[:],
-                            scalar=gain_col,
-                            in1=xn_sb[:, load * LOAD_POS + lo : load * LOAD_POS + lo + BANK_POS],
-                            op0=ALU.mult,
-                            op1=ALU.add,
-                        )
+        def add_bias(j):
+            y[j] = work_pool.tile([P, BANK], F32, name="y")
+            nc.scalar.activation(out=y[j][:], in_=z[j][:], func=ACT.Identity, bias=bias_col)
 
-                nc.sync.dma_start(out=out_view[b, :, load_cols], in_=out_sb[:])
+        def to_positions(j):
+            y_t[j] = yt_psum.tile([P, BLOCKS, BLOCK], F32, name="y_t")
+            for i in range(BLOCKS):
+                nc.tensor.transpose(y_t[j][:, i, :], y[j][:, i * BLOCK : (i + 1) * BLOCK], identity[:])
+
+        def statistics(j):
+            stats = small_pool.tile([P, BLOCKS, 6], F32, name="stats")
+            mean_var[j] = small_pool.tile([P, BLOCKS, 2], F32, name="mean_var")
+            for i in range(BLOCKS):
+                nc.vector.bn_stats(out=stats[:, i, :], in_=y_t[j][:, i, :])
+            for i in range(BLOCKS):
+                nc.vector.bn_aggr(out=mean_var[j][:, i, :], in_=stats[:, i, :])
+
+        def root(j):
+            rstd[j] = small_pool.tile([P, BLOCKS], F32, name="rstd")
+            nc.scalar.activation(
+                out=rstd[j][:], in_=mean_var[j][:, :, 1], func=ACT.Abs_reciprocal_sqrt, bias=eps_col[:]
+            )
+
+        def scale_and_shift(j):
+            shift[j] = small_pool.tile([P, BLOCKS], F32, name="shift")
+            nc.vector.scalar_tensor_tensor(
+                out=shift[j][:], in0=mean_var[j][:, :, 0], scalar=-1.0, in1=rstd[j][:], op0=ALU.mult, op1=ALU.mult
+            )
+
+        def normalise(j):
+            normed[j] = work_pool.tile([P, BLOCKS, BLOCK], F32, name="normed")
+            for i in range(BLOCKS):
+                nc.scalar.activation(
+                    out=normed[j][:, i, :],
+                    in_=y_t[j][:, i, :],
+                    func=ACT.Identity,
+                    scale=rstd[j][:, i : i + 1],
+                    bias=shift[j][:, i : i + 1],
+                )
+
+        def to_channels(j):
+            u_t[j] = ut_psum.tile([P, BANK], F32, name="u_t")
+            for i in range(BLOCKS):
+                nc.tensor.transpose(u_t[j][:, i * BLOCK : (i + 1) * BLOCK], normed[j][:, i, :], identity[:])
+
+        def finish(j):
+            group = j // STORE_BANKS
+            part = j % STORE_BANKS
+            if part == 0:
+                out_sb[group] = out_pool.tile([P, STORE_BANKS * BANK], F32, name="out_sb")
+            b = j // BANKS_PER_IMAGE
+            lo = (j % BANKS_PER_IMAGE) * BANK
+            nc.vector.scalar_tensor_tensor(
+                out=out_sb[group][:, part * BANK : (part + 1) * BANK],
+                in0=u_t[j][:],
+                scalar=gain_col,
+                in1=xn_of_image[b][:, lo : lo + BANK],
+                op0=ALU.mult,
+                op1=ALU.add,
+            )
+            if part == STORE_BANKS - 1:
+                first = lo - (STORE_BANKS - 1) * BANK
+                nc.sync.dma_start(out=out_view[b, :, first : lo + BANK], in_=out_sb[group][:])
+
+        ctx.enter_context(tc.manual_schedule())
+
+        for j in range(GROUPED_BUFS):
+            regroup_scalar(j)
+            regroup_gpsimd(j)
+
+        for s in range(N_BANKS + 5):
+            if ok(s - 3):
+                scale_and_shift(s - 3)
+            if ok(s):
+                quantise(s)
+            if ok(s - 1):
+                add_bias(s - 1)
+            if ok(s - 4):
+                to_channels(s - 4)
+            if ok(s - 1):
+                to_positions(s - 1)
+            if ok(s):
+                project(s)
+            ahead = s + GROUPED_BUFS
+            if ok(ahead):
+                regroup_scalar(ahead)
+                regroup_gpsimd(ahead)
+            if ok(s - 2):
+                statistics(s - 2)
+            if ok(s - 3):
+                normalise(s - 3)
+            if ok(s - 2):
+                root(s - 2)
+            if ok(s - 4):
+                finish(s - 4)
+            if ok(ahead):
+                if ahead % LOAD_BANKS == LOAD_BANKS - 1 and ahead >= 2 * LOAD_BANKS - 1:
+                    k = ahead // LOAD_BANKS + RAW_BUFS
+                    if k < N_LOADS:
+                        load_raw(k)
+            done = s - 4
+            if ok(done) and done % BANKS_PER_IMAGE == BANKS_PER_IMAGE - 1:
+                b = done // BANKS_PER_IMAGE + 2
+                if b < IMAGES:
+                    load_xn(b)

@@ -24,10 +24,8 @@ BLOCK = 128
 BLOCKS = BANK // BLOCK
 BANKS_PER_IMAGE = POSITIONS // BANK
 N_BANKS = IMAGES * BANKS_PER_IMAGE
-LOAD_BANKS = 4
-N_LOADS = N_BANKS // LOAD_BANKS
-RAW_BUFS = 3
-STORE_BANKS = 2
+HEAD_BANKS = 4
+TAIL_STORE_BANKS = 2
 GROUPED_BUFS = 2
 SCALAR_POS = 224
 GPSIMD_POS = BANK - SCALAR_POS
@@ -43,8 +41,9 @@ def tile_linearattention_pb_t_kernel(tc, h_attn, xn, Wout_words, Wout_scales, bo
 
     with ExitStack() as ctx:
         const = ctx.enter_context(tc.tile_pool(name="const", bufs=1))
-        head_pool = ctx.enter_context(tc.tile_pool(name="head", bufs=LOAD_BANKS))
-        raw_pool = ctx.enter_context(tc.tile_pool(name="raw", bufs=RAW_BUFS))
+        head_pool = ctx.enter_context(tc.tile_pool(name="head", bufs=HEAD_BANKS))
+        rest_pool = ctx.enter_context(tc.tile_pool(name="rest", bufs=1))
+        raw_pool = ctx.enter_context(tc.tile_pool(name="raw", bufs=IMAGES - 1))
         xn_pool = ctx.enter_context(tc.tile_pool(name="xn", bufs=2))
 
         raw_of_bank = {}
@@ -54,14 +53,17 @@ def tile_linearattention_pb_t_kernel(tc, h_attn, xn, Wout_words, Wout_scales, bo
             nc.sync.dma_start(out=t[:], in_=a_view[0, :, :, j * BANK : (j + 1) * BANK])
             raw_of_bank[j] = t[:]
 
-        def load_raw(k):
-            t = raw_pool.tile([P, PACK, LOAD_BANKS * BANK], BF16, name="raw")
-            first = k * LOAD_BANKS
-            b = first // BANKS_PER_IMAGE
-            lo = (first % BANKS_PER_IMAGE) * BANK
-            nc.sync.dma_start(out=t[:], in_=a_view[b, :, :, lo : lo + LOAD_BANKS * BANK])
-            for i in range(LOAD_BANKS):
-                raw_of_bank[first + i] = t[:, :, i * BANK : (i + 1) * BANK]
+        def load_rest():
+            t = rest_pool.tile([P, PACK, POSITIONS - HEAD_BANKS * BANK], BF16, name="rest")
+            nc.sync.dma_start(out=t[:], in_=a_view[0, :, :, HEAD_BANKS * BANK : POSITIONS])
+            for i in range(BANKS_PER_IMAGE - HEAD_BANKS):
+                raw_of_bank[HEAD_BANKS + i] = t[:, :, i * BANK : (i + 1) * BANK]
+
+        def load_raw(b):
+            t = raw_pool.tile([P, PACK, POSITIONS], BF16, name="raw")
+            nc.sync.dma_start(out=t[:], in_=a_view[b])
+            for i in range(BANKS_PER_IMAGE):
+                raw_of_bank[b * BANKS_PER_IMAGE + i] = t[:, :, i * BANK : (i + 1) * BANK]
 
         xn_of_image = {}
 
@@ -96,11 +98,12 @@ def tile_linearattention_pb_t_kernel(tc, h_attn, xn, Wout_words, Wout_scales, bo
         nc.sync.dma_start(out=rows_bf[1:2, :], in_=outnorm_g.rearrange("o c h w -> o (c h w)"))
         load_head(2)
         load_head(3)
-        load_raw(1)
+        load_rest()
         load_xn(0)
+        load_raw(1)
+        load_xn(1)
         load_raw(2)
         load_raw(3)
-        load_xn(1)
         rows_f32 = const.tile([P, P], F32)
         nc.vector.tensor_copy(out=rows_f32[:], in_=rows_bf[:])
         per_channel = const.tile([P, 2], F32)
@@ -115,7 +118,7 @@ def tile_linearattention_pb_t_kernel(tc, h_attn, xn, Wout_words, Wout_scales, bo
         quant_pool = ctx.enter_context(tc.tile_pool(name="quant", bufs=3))
         work_pool = ctx.enter_context(tc.tile_pool(name="work", bufs=3))
         small_pool = ctx.enter_context(tc.tile_pool(name="small", bufs=6))
-        out_pool = ctx.enter_context(tc.tile_pool(name="outs", bufs=3))
+        out_pool = ctx.enter_context(tc.tile_pool(name="outs", bufs=2))
         z_psum = ctx.enter_context(tc.psum_pool(name="z_psum", bufs=2))
         yt_psum = ctx.enter_context(tc.psum_pool(name="yt_psum", bufs=4))
         ut_psum = ctx.enter_context(tc.psum_pool(name="ut_psum", bufs=2))
@@ -215,23 +218,25 @@ def tile_linearattention_pb_t_kernel(tc, h_attn, xn, Wout_words, Wout_scales, bo
                 nc.tensor.transpose(u_t[j][:, i * BLOCK : (i + 1) * BLOCK], normed[j][:, i, :], identity[:])
 
         def finish(j):
-            group = j // STORE_BANKS
-            part = j % STORE_BANKS
-            if part == 0:
-                out_sb[group] = out_pool.tile([P, STORE_BANKS * BANK], F32, name="out_sb")
             b = j // BANKS_PER_IMAGE
             lo = (j % BANKS_PER_IMAGE) * BANK
+            if lo == 0:
+                out_sb[b] = out_pool.tile([P, POSITIONS], F32, name="out_sb")
             nc.vector.scalar_tensor_tensor(
-                out=out_sb[group][:, part * BANK : (part + 1) * BANK],
+                out=out_sb[b][:, lo : lo + BANK],
                 in0=u_t[j][:],
                 scalar=gain_col,
                 in1=xn_of_image[b][:, lo : lo + BANK],
                 op0=ALU.mult,
                 op1=ALU.add,
             )
-            if part == STORE_BANKS - 1:
-                first = lo - (STORE_BANKS - 1) * BANK
-                nc.sync.dma_start(out=out_view[b, :, first : lo + BANK], in_=out_sb[group][:])
+            hi = lo + BANK
+            if b < IMAGES - 1:
+                if hi == POSITIONS:
+                    nc.sync.dma_start(out=out_view[b], in_=out_sb[b][:])
+            elif hi % (TAIL_STORE_BANKS * BANK) == 0:
+                first = hi - TAIL_STORE_BANKS * BANK
+                nc.sync.dma_start(out=out_view[b, :, first:hi], in_=out_sb[b][:, first:hi])
 
         ctx.enter_context(tc.manual_schedule())
 
@@ -264,11 +269,6 @@ def tile_linearattention_pb_t_kernel(tc, h_attn, xn, Wout_words, Wout_scales, bo
                 root(s - 2)
             if ok(s - 4):
                 finish(s - 4)
-            if ok(ahead):
-                if ahead % LOAD_BANKS == LOAD_BANKS - 1 and ahead >= 2 * LOAD_BANKS - 1:
-                    k = ahead // LOAD_BANKS + RAW_BUFS
-                    if k < N_LOADS:
-                        load_raw(k)
             done = s - 4
             if ok(done) and done % BANKS_PER_IMAGE == BANKS_PER_IMAGE - 1:
                 b = done // BANKS_PER_IMAGE + 2

@@ -27,8 +27,9 @@ N_BANKS = IMAGES * BANKS_PER_IMAGE
 HEAD_BANKS = 4
 TAIL_STORE_BANKS = 2
 GROUPED_BUFS = 2
-SCALAR_POS = 224
-GPSIMD_POS = BANK - SCALAR_POS
+SCALAR_POS = 240
+GPSIMD_POS = 128
+VECTOR_POS = BANK - SCALAR_POS - GPSIMD_POS
 
 FLOPS = 2 * 512 * P * IMAGES * POSITIONS
 
@@ -142,14 +143,20 @@ def tile_linearattention_pb_t_kernel(tc, h_attn, xn, Wout_words, Wout_scales, bo
 
         def regroup_gpsimd(j):
             hi = SCALAR_POS + GPSIMD_POS
+            dst, src = runs_of_4(grouped[j][:, SCALAR_POS:hi, :], raw_of_bank[j][:, :, SCALAR_POS:hi])
             nc.gpsimd.tensor_scalar(
-                out=grouped[j][:, SCALAR_POS:hi, :],
-                in0=raw_of_bank[j][:, :, SCALAR_POS:hi].rearrange("p t w -> p w t"),
+                out=dst,
+                in0=src,
                 scalar1=1.0,
                 scalar2=0.0,
                 op0=ALU.mult,
                 op1=ALU.add,
             )
+
+        def regroup_vector(j):
+            lo = SCALAR_POS + GPSIMD_POS
+            dst, src = runs_of_4(grouped[j][:, lo:BANK, :], raw_of_bank[j][:, :, lo:BANK])
+            nc.vector.tensor_copy(out=dst, in_=src)
 
         def quantise(j):
             codes[j] = quant_pool.tile([P, BANK], U32, align_bytes=64, name="codes")
@@ -243,6 +250,7 @@ def tile_linearattention_pb_t_kernel(tc, h_attn, xn, Wout_words, Wout_scales, bo
         for j in range(GROUPED_BUFS):
             regroup_scalar(j)
             regroup_gpsimd(j)
+            regroup_vector(j)
 
         for s in range(N_BANKS + 5):
             if ok(s - 3):
@@ -269,6 +277,8 @@ def tile_linearattention_pb_t_kernel(tc, h_attn, xn, Wout_words, Wout_scales, bo
                 root(s - 2)
             if ok(s - 4):
                 finish(s - 4)
+            if ok(ahead):
+                regroup_vector(ahead)
             done = s - 4
             if ok(done) and done % BANKS_PER_IMAGE == BANKS_PER_IMAGE - 1:
                 b = done // BANKS_PER_IMAGE + 2

@@ -27,7 +27,7 @@ N_BANKS = IMAGES * BANKS_PER_IMAGE
 HEAD_BANKS = 4
 TAIL_STORE_BANKS = 2
 GROUPED_BUFS = 2
-SCALAR_POS = 240
+SCALAR_POS = 112
 GPSIMD_POS = 128
 VECTOR_POS = BANK - SCALAR_POS - GPSIMD_POS
 

@@ -26,10 +26,9 @@ BANKS_PER_IMAGE = POSITIONS // BANK
 N_BANKS = IMAGES * BANKS_PER_IMAGE
 HEAD_BANKS = 4
 TAIL_STORE_BANKS = 2
-GROUPED_BUFS = 2
-SCALAR_POS = 112
-GPSIMD_POS = 128
-VECTOR_POS = BANK - SCALAR_POS - GPSIMD_POS
+GROUPED_BUFS = 3
+SCALAR_POS = 224
+GPSIMD_POS = BANK - SCALAR_POS
 
 FLOPS = 2 * 512 * P * IMAGES * POSITIONS
 
@@ -137,26 +136,20 @@ def tile_linearattention_pb_t_kernel(tc, h_attn, xn, Wout_words, Wout_scales, bo
             )
 
         def regroup_scalar(j):
-            grouped[j] = grouped_pool.tile([P, BANK, PACK], BF16, align_bytes=64, name="grouped")
             dst, src = runs_of_4(grouped[j][:, 0:SCALAR_POS, :], raw_of_bank[j][:, :, 0:SCALAR_POS])
             nc.scalar.copy(out=dst, in_=src)
 
         def regroup_gpsimd(j):
+            grouped[j] = grouped_pool.tile([P, BANK, PACK], BF16, align_bytes=64, name="grouped")
             hi = SCALAR_POS + GPSIMD_POS
-            dst, src = runs_of_4(grouped[j][:, SCALAR_POS:hi, :], raw_of_bank[j][:, :, SCALAR_POS:hi])
             nc.gpsimd.tensor_scalar(
-                out=dst,
-                in0=src,
+                out=grouped[j][:, SCALAR_POS:hi, :],
+                in0=raw_of_bank[j][:, :, SCALAR_POS:hi].rearrange("p t w -> p w t"),
                 scalar1=1.0,
                 scalar2=0.0,
                 op0=ALU.mult,
                 op1=ALU.add,
             )
-
-        def regroup_vector(j):
-            lo = SCALAR_POS + GPSIMD_POS
-            dst, src = runs_of_4(grouped[j][:, lo:BANK, :], raw_of_bank[j][:, :, lo:BANK])
-            nc.vector.tensor_copy(out=dst, in_=src)
 
         def quantise(j):
             codes[j] = quant_pool.tile([P, BANK], U32, align_bytes=64, name="codes")
@@ -247,39 +240,37 @@ def tile_linearattention_pb_t_kernel(tc, h_attn, xn, Wout_words, Wout_scales, bo
 
         ctx.enter_context(tc.manual_schedule())
 
-        for j in range(GROUPED_BUFS):
-            regroup_scalar(j)
+        for j in range(3):
             regroup_gpsimd(j)
-            regroup_vector(j)
+        for j in range(2):
+            regroup_scalar(j)
 
-        for s in range(N_BANKS + 5):
-            if ok(s - 3):
-                scale_and_shift(s - 3)
+        for s in range(N_BANKS + 6):
             if ok(s):
                 quantise(s)
             if ok(s - 1):
                 add_bias(s - 1)
-            if ok(s - 4):
-                to_channels(s - 4)
+            if ok(s - 5):
+                to_channels(s - 5)
             if ok(s - 1):
                 to_positions(s - 1)
             if ok(s):
                 project(s)
-            ahead = s + GROUPED_BUFS
-            if ok(ahead):
-                regroup_scalar(ahead)
-                regroup_gpsimd(ahead)
+            if ok(s + 3):
+                regroup_gpsimd(s + 3)
+            if ok(s + 2):
+                regroup_scalar(s + 2)
             if ok(s - 2):
                 statistics(s - 2)
-            if ok(s - 3):
-                normalise(s - 3)
+            if ok(s - 4):
+                normalise(s - 4)
             if ok(s - 2):
                 root(s - 2)
-            if ok(s - 4):
-                finish(s - 4)
-            if ok(ahead):
-                regroup_vector(ahead)
-            done = s - 4
+            if ok(s - 5):
+                finish(s - 5)
+            if ok(s - 3):
+                scale_and_shift(s - 3)
+            done = s - 5
             if ok(done) and done % BANKS_PER_IMAGE == BANKS_PER_IMAGE - 1:
                 b = done // BANKS_PER_IMAGE + 2
                 if b < IMAGES:

@@ -27,7 +27,7 @@ N_BANKS = IMAGES * BANKS_PER_IMAGE
 HEAD_BANKS = 4
 TAIL_STORE_BANKS = 2
 GROUPED_BUFS = 3
-SCALAR_POS = 224
+SCALAR_POS = 160
 GPSIMD_POS = BANK - SCALAR_POS
 
 FLOPS = 2 * 512 * P * IMAGES * POSITIONS

@@ -27,7 +27,8 @@ N_BANKS = IMAGES * BANKS_PER_IMAGE
 HEAD_BANKS = 4
 TAIL_STORE_BANKS = 2
 GROUPED_BUFS = 3
-SCALAR_POS = 160
+PROJECT_REPEATS = 4
+SCALAR_POS = 192
 GPSIMD_POS = BANK - SCALAR_POS
 
 FLOPS = 2 * 512 * P * IMAGES * POSITIONS
@@ -162,15 +163,16 @@ def tile_linearattention_pb_t_kernel(tc, h_attn, xn, Wout_words, Wout_scales, bo
 
         def project(j):
             z[j] = z_psum.tile([P, BANK], F32, name="z")
-            nc.tensor.matmul_mx(
-                out=z[j][:],
-                lhsT=w_words[:].bitcast(FP4X4),
-                lhsT_scale=w_plane[:],
-                rhs=codes[j][:].bitcast(FP8X4),
-                rhs_scale=scales[j][:],
-                start=True,
-                stop=True,
-            )
+            for repeat in range(PROJECT_REPEATS):
+                nc.tensor.matmul_mx(
+                    out=z[j][:],
+                    lhsT=w_words[:].bitcast(FP4X4),
+                    lhsT_scale=w_plane[:],
+                    rhs=codes[j][:].bitcast(FP8X4),
+                    rhs_scale=scales[j][:],
+                    start=True,
+                    stop=True,
+                )
 
         def add_bias(j):
             y[j] = work_pool.tile([P, BANK], F32, name="y")
@@ -252,10 +254,10 @@ def tile_linearattention_pb_t_kernel(tc, h_attn, xn, Wout_words, Wout_scales, bo
                 add_bias(s - 1)
             if ok(s - 5):
                 to_channels(s - 5)
-            if ok(s - 1):
-                to_positions(s - 1)
             if ok(s):
                 project(s)
+            if ok(s - 1):
+                to_positions(s - 1)
             if ok(s + 3):
                 regroup_gpsimd(s + 3)
             if ok(s + 2):

@@ -27,7 +27,7 @@ N_BANKS = IMAGES * BANKS_PER_IMAGE
 HEAD_BANKS = 4
 TAIL_STORE_BANKS = 2
 GROUPED_BUFS = 3
-PROJECT_REPEATS = 4
+PROJECT_REPEATS = 1
 SCALAR_POS = 192
 GPSIMD_POS = BANK - SCALAR_POS
 

@@ -125,7 +125,7 @@ def tile_linearattention_pb_t_kernel(tc, h_attn, xn, Wout_words, Wout_scales, bo
         ut_psum = ctx.enter_context(tc.psum_pool(name="ut_psum", bufs=2))
 
         grouped, codes, scales, z, y, y_t = {}, {}, {}, {}, {}, {}
-        mean_var, rstd, shift, normed, u_t, out_sb = {}, {}, {}, {}, {}, {}
+        stats, rstd, shift, normed, u_t, out_sb = {}, {}, {}, {}, {}, {}
 
         def ok(j):
             return 0 <= j < N_BANKS
@@ -184,23 +184,23 @@ def tile_linearattention_pb_t_kernel(tc, h_attn, xn, Wout_words, Wout_scales, bo
                 nc.tensor.transpose(y_t[j][:, i, :], y[j][:, i * BLOCK : (i + 1) * BLOCK], identity[:])
 
         def statistics(j):
-            stats = small_pool.tile([P, BLOCKS, 6], F32, name="stats")
-            mean_var[j] = small_pool.tile([P, BLOCKS, 2], F32, name="mean_var")
-            for i in range(BLOCKS):
-                nc.vector.bn_stats(out=stats[:, i, :], in_=y_t[j][:, i, :])
-            for i in range(BLOCKS):
-                nc.vector.bn_aggr(out=mean_var[j][:, i, :], in_=stats[:, i, :])
+            stats[j] = small_pool.tile([P, BLOCKS, 3], F32, name="stats")
+            for i in range(0, BLOCKS, 2):
+                nc.vector.bn_stats(
+                    out=stats[j][:, i : i + 2, :].rearrange("p b f -> p (b f)"),
+                    in_=y_t[j][:, i : i + 2, :].rearrange("p b c -> p c b"),
+                )
 
         def root(j):
             rstd[j] = small_pool.tile([P, BLOCKS], F32, name="rstd")
             nc.scalar.activation(
-                out=rstd[j][:], in_=mean_var[j][:, :, 1], func=ACT.Abs_reciprocal_sqrt, bias=eps_col[:]
+                out=rstd[j][:], in_=stats[j][:, :, 2], func=ACT.Abs_reciprocal_sqrt, scale=1.0 / P, bias=eps_col[:]
             )
 
         def scale_and_shift(j):
             shift[j] = small_pool.tile([P, BLOCKS], F32, name="shift")
             nc.vector.scalar_tensor_tensor(
-                out=shift[j][:], in0=mean_var[j][:, :, 0], scalar=-1.0, in1=rstd[j][:], op0=ALU.mult, op1=ALU.mult
+                out=shift[j][:], in0=stats[j][:, :, 1], scalar=-1.0, in1=rstd[j][:], op0=ALU.mult, op1=ALU.mult
             )
 
         def normalise(j):

@@ -28,8 +28,9 @@ HEAD_BANKS = 4
 TAIL_STORE_BANKS = 2
 GROUPED_BUFS = 3
 PROJECT_REPEATS = 1
-SCALAR_POS = 192
-GPSIMD_POS = BANK - SCALAR_POS
+SCALAR_POS = 160
+VECTOR_POS = 160
+GPSIMD_POS = BANK - SCALAR_POS - VECTOR_POS
 
 FLOPS = 2 * 512 * P * IMAGES * POSITIONS
 
@@ -130,26 +131,29 @@ def tile_linearattention_pb_t_kernel(tc, h_attn, xn, Wout_words, Wout_scales, bo
         def ok(j):
             return 0 <= j < N_BANKS
 
-        def runs_of_4(dst, src):
-            return (
-                dst.rearrange("p (c i) t -> p c t i", i=4),
-                src.rearrange("p t (c i) -> p c t i", i=4),
-            )
-
         def regroup_scalar(j):
-            dst, src = runs_of_4(grouped[j][:, 0:SCALAR_POS, :], raw_of_bank[j][:, :, 0:SCALAR_POS])
-            nc.scalar.copy(out=dst, in_=src)
+            nc.scalar.copy(
+                out=grouped[j][:, 0:SCALAR_POS, :],
+                in_=raw_of_bank[j][:, :, 0:SCALAR_POS].rearrange("p t w -> p w t"),
+            )
 
         def regroup_gpsimd(j):
             grouped[j] = grouped_pool.tile([P, BANK, PACK], BF16, align_bytes=64, name="grouped")
-            hi = SCALAR_POS + GPSIMD_POS
+            lo = SCALAR_POS + VECTOR_POS
             nc.gpsimd.tensor_scalar(
-                out=grouped[j][:, SCALAR_POS:hi, :],
-                in0=raw_of_bank[j][:, :, SCALAR_POS:hi].rearrange("p t w -> p w t"),
+                out=grouped[j][:, lo:BANK, :],
+                in0=raw_of_bank[j][:, :, lo:BANK].rearrange("p t w -> p w t"),
                 scalar1=1.0,
                 scalar2=0.0,
                 op0=ALU.mult,
                 op1=ALU.add,
+            )
+
+        def regroup_vector(j):
+            hi = SCALAR_POS + VECTOR_POS
+            nc.vector.tensor_copy(
+                out=grouped[j][:, SCALAR_POS:hi, :],
+                in_=raw_of_bank[j][:, :, SCALAR_POS:hi].rearrange("p t w -> p w t"),
             )
 
         def quantise(j):
@@ -246,8 +250,11 @@ def tile_linearattention_pb_t_kernel(tc, h_attn, xn, Wout_words, Wout_scales, bo
             regroup_gpsimd(j)
         for j in range(2):
             regroup_scalar(j)
+            regroup_vector(j)
 
         for s in range(N_BANKS + 6):
+            if ok(s + 2):
+                regroup_vector(s + 2)
             if ok(s):
                 quantise(s)
             if ok(s - 1):

@@ -131,6 +131,9 @@ def tile_linearattention_pb_t_kernel(tc, h_attn, xn, Wout_words, Wout_scales, bo
         def ok(j):
             return 0 <= j < N_BANKS
 
+        def vector_end(j):
+            return BANK if j < HEAD_BANKS else SCALAR_POS + VECTOR_POS
+
         def regroup_scalar(j):
             nc.scalar.copy(
                 out=grouped[j][:, 0:SCALAR_POS, :],
@@ -139,18 +142,19 @@ def tile_linearattention_pb_t_kernel(tc, h_attn, xn, Wout_words, Wout_scales, bo
 
         def regroup_gpsimd(j):
             grouped[j] = grouped_pool.tile([P, BANK, PACK], BF16, align_bytes=64, name="grouped")
-            lo = SCALAR_POS + VECTOR_POS
-            nc.gpsimd.tensor_scalar(
-                out=grouped[j][:, lo:BANK, :],
-                in0=raw_of_bank[j][:, :, lo:BANK].rearrange("p t w -> p w t"),
-                scalar1=1.0,
-                scalar2=0.0,
-                op0=ALU.mult,
-                op1=ALU.add,
-            )
+            lo = vector_end(j)
+            if lo < BANK:
+                nc.gpsimd.tensor_scalar(
+                    out=grouped[j][:, lo:BANK, :],
+                    in0=raw_of_bank[j][:, :, lo:BANK].rearrange("p t w -> p w t"),
+                    scalar1=1.0,
+                    scalar2=0.0,
+                    op0=ALU.mult,
+                    op1=ALU.add,
+                )
 
         def regroup_vector(j):
-            hi = SCALAR_POS + VECTOR_POS
+            hi = vector_end(j)
             nc.vector.tensor_copy(
                 out=grouped[j][:, SCALAR_POS:hi, :],
                 in_=raw_of_bank[j][:, :, SCALAR_POS:hi].rearrange("p t w -> p w t"),
@@ -250,11 +254,9 @@ def tile_linearattention_pb_t_kernel(tc, h_attn, xn, Wout_words, Wout_scales, bo
             regroup_gpsimd(j)
         for j in range(2):
             regroup_scalar(j)
-            regroup_vector(j)
+        regroup_vector(0)
 
         for s in range(N_BANKS + 6):
-            if ok(s + 2):
-                regroup_vector(s + 2)
             if ok(s):
                 quantise(s)
             if ok(s - 1):
@@ -279,6 +281,10 @@ def tile_linearattention_pb_t_kernel(tc, h_attn, xn, Wout_words, Wout_scales, bo
                 finish(s - 5)
             if ok(s - 3):
                 scale_and_shift(s - 3)
+            if s == 0:
+                regroup_vector(1)
+            if ok(s + 2):
+                regroup_vector(s + 2)
             done = s - 5
             if ok(done) and done % BANKS_PER_IMAGE == BANKS_PER_IMAGE - 1:
                 b = done // BANKS_PER_IMAGE + 2

@@ -28,8 +28,8 @@ HEAD_BANKS = 4
 TAIL_STORE_BANKS = 2
 GROUPED_BUFS = 3
 PROJECT_REPEATS = 1
-SCALAR_POS = 160
-VECTOR_POS = 160
+SCALAR_POS = 176
+VECTOR_POS = 132
 GPSIMD_POS = BANK - SCALAR_POS - VECTOR_POS
 
 FLOPS = 2 * 512 * P * IMAGES * POSITIONS

@@ -25,7 +25,6 @@ BLOCKS = BANK // BLOCK
 BANKS_PER_IMAGE = POSITIONS // BANK
 N_BANKS = IMAGES * BANKS_PER_IMAGE
 HEAD_BANKS = 4
-TAIL_STORE_BANKS = 2
 GROUPED_BUFS = 3
 PROJECT_REPEATS = 1
 SCALAR_POS = 176
@@ -232,21 +231,22 @@ def tile_linearattention_pb_t_kernel(tc, h_attn, xn, Wout_words, Wout_scales, bo
             lo = (j % BANKS_PER_IMAGE) * BANK
             if lo == 0:
                 out_sb[b] = out_pool.tile([P, POSITIONS], F32, name="out_sb")
-            nc.vector.scalar_tensor_tensor(
-                out=out_sb[b][:, lo : lo + BANK],
-                in0=u_t[j][:],
-                scalar=gain_col,
-                in1=xn_of_image[b][:, lo : lo + BANK],
-                op0=ALU.mult,
-                op1=ALU.add,
-            )
-            hi = lo + BANK
-            if b < IMAGES - 1:
-                if hi == POSITIONS:
-                    nc.sync.dma_start(out=out_view[b], in_=out_sb[b][:])
-            elif hi % (TAIL_STORE_BANKS * BANK) == 0:
-                first = hi - TAIL_STORE_BANKS * BANK
-                nc.sync.dma_start(out=out_view[b, :, first:hi], in_=out_sb[b][:, first:hi])
+            pieces = 2 if j == N_BANKS - 1 else 1
+            width = BANK // pieces
+            for piece in range(pieces):
+                first = lo + piece * width
+                nc.vector.scalar_tensor_tensor(
+                    out=out_sb[b][:, first : first + width],
+                    in0=u_t[j][:, piece * width : (piece + 1) * width],
+                    scalar=gain_col,
+                    in1=xn_of_image[b][:, first : first + width],
+                    op0=ALU.mult,
+                    op1=ALU.add,
+                )
+                if b == IMAGES - 1:
+                    nc.sync.dma_start(out=out_view[b, :, first : first + width], in_=out_sb[b][:, first : first + width])
+            if b < IMAGES - 1 and lo + BANK == POSITIONS:
+                nc.sync.dma_start(out=out_view[b], in_=out_sb[b][:])
 
         ctx.enter_context(tc.manual_schedule())
 

from contextlib import ExitStack

import concourse.mybir as mybir
from concourse.masks import make_identity

F32 = mybir.dt.float32
BF16 = mybir.dt.bfloat16
I32 = mybir.dt.int32
U32 = mybir.dt.uint32
U8 = mybir.dt.uint8
FP8X4 = mybir.dt.float8_e4m3fn_x4
FP4X4 = mybir.dt.float4_e2m1fn_x4
ACT = mybir.ActivationFunctionType
ALU = mybir.AluOpType

P = 128
PACK = 4
IMAGES = 4
POSITIONS = 64 * 64
EPS = 1e-5

BANK = 512
BLOCK = 128
BLOCKS = BANK // BLOCK
BANKS_PER_IMAGE = POSITIONS // BANK
N_BANKS = IMAGES * BANKS_PER_IMAGE
HEAD_BANKS = 4
GROUPED_BUFS = 3
PROJECT_REPEATS = 1
SCALAR_POS = 176
VECTOR_POS = 132
GPSIMD_POS = BANK - SCALAR_POS - VECTOR_POS

FLOPS = 2 * 512 * P * IMAGES * POSITIONS


def tile_linearattention_pb_t_kernel(tc, h_attn, xn, Wout_words, Wout_scales, bout, outnorm_g, out):
    nc = tc.nc
    a_view = h_attn.rearrange("b (p t) h w -> b p t (h w)", t=PACK)
    xn_view = xn.rearrange("b c h w -> b c (h w)")
    out_view = out.rearrange("b c h w -> b c (h w)")

    with ExitStack() as ctx:
        const = ctx.enter_context(tc.tile_pool(name="const", bufs=1))
        head_pool = ctx.enter_context(tc.tile_pool(name="head", bufs=HEAD_BANKS))
        rest_pool = ctx.enter_context(tc.tile_pool(name="rest", bufs=1))
        raw_pool = ctx.enter_context(tc.tile_pool(name="raw", bufs=IMAGES - 1))
        xn_pool = ctx.enter_context(tc.tile_pool(name="xn", bufs=2))

        raw_of_bank = {}

        def load_head(j):
            t = head_pool.tile([P, PACK, BANK], BF16, name="head")
            nc.sync.dma_start(out=t[:], in_=a_view[0, :, :, j * BANK : (j + 1) * BANK])
            raw_of_bank[j] = t[:]

        def load_rest():
            t = rest_pool.tile([P, PACK, POSITIONS - HEAD_BANKS * BANK], BF16, name="rest")
            nc.sync.dma_start(out=t[:], in_=a_view[0, :, :, HEAD_BANKS * BANK : POSITIONS])
            for i in range(BANKS_PER_IMAGE - HEAD_BANKS):
                raw_of_bank[HEAD_BANKS + i] = t[:, :, i * BANK : (i + 1) * BANK]

        def load_raw(b):
            t = raw_pool.tile([P, PACK, POSITIONS], BF16, name="raw")
            nc.sync.dma_start(out=t[:], in_=a_view[b])
            for i in range(BANKS_PER_IMAGE):
                raw_of_bank[b * BANKS_PER_IMAGE + i] = t[:, :, i * BANK : (i + 1) * BANK]

        xn_of_image = {}

        def load_xn(b):
            t = xn_pool.tile([P, POSITIONS], BF16, name="xn_sb")
            nc.sync.dma_start(out=t[:], in_=xn_view[b])
            xn_of_image[b] = t

        load_head(0)
        load_head(1)

        w_words = const.tile([P, 2 * P], U8, align_bytes=64)
        nc.sync.dma_start(out=w_words[:].bitcast(I32), in_=Wout_words[0].bitcast(I32))
        w_plane = const.tile([P, P], U8, align_bytes=64)
        nc.vector.memset(w_plane[:].bitcast(I32), 0)
        for quadrant in range(4):
            nc.sync.dma_start(
                out=w_plane[32 * quadrant : 32 * quadrant + 4, :].bitcast(I32),
                in_=Wout_scales[0, 4 * quadrant : 4 * quadrant + 4, :].bitcast(I32),
            )

        identity = const.tile([P, P], F32)
        make_identity(nc, identity[:])
        eps_col = const.tile([P, 1], F32)
        nc.vector.memset(eps_col[:], EPS)
        warm = const.tile([P, 1], F32)
        nc.scalar.activation(out=warm[:], in_=eps_col[:], func=ACT.Abs_reciprocal_sqrt)

        rows_bf = const.tile([P, P], BF16)
        nc.vector.memset(rows_bf[:], 0.0)
        nc.sync.dma_start(out=rows_bf[0:1, :], in_=bout.unsqueeze(0))
        nc.sync.dma_start(out=rows_bf[1:2, :], in_=outnorm_g.rearrange("o c h w -> o (c h w)"))
        load_head(2)
        load_head(3)
        load_rest()
        load_xn(0)
        load_raw(1)
        load_xn(1)
        load_raw(2)
        load_raw(3)
        rows_f32 = const.tile([P, P], F32)
        nc.vector.tensor_copy(out=rows_f32[:], in_=rows_bf[:])
        per_channel = const.tile([P, 2], F32)
        with tc.psum_pool(name="setup_psum", bufs=1) as setup_psum:
            cols_ps = setup_psum.tile([P, P], F32)
            nc.tensor.transpose(cols_ps[:], rows_f32[:], identity[:])
            nc.vector.tensor_copy(out=per_channel[:], in_=cols_ps[:, 0:2])
        bias_col = per_channel[:, 0:1]
        gain_col = per_channel[:, 1:2]

        grouped_pool = ctx.enter_context(tc.tile_pool(name="grouped", bufs=GROUPED_BUFS))
        quant_pool = ctx.enter_context(tc.tile_pool(name="quant", bufs=3))
        work_pool = ctx.enter_context(tc.tile_pool(name="work", bufs=3))
        small_pool = ctx.enter_context(tc.tile_pool(name="small", bufs=6))
        out_pool = ctx.enter_context(tc.tile_pool(name="outs", bufs=2))
        z_psum = ctx.enter_context(tc.psum_pool(name="z_psum", bufs=2))
        yt_psum = ctx.enter_context(tc.psum_pool(name="yt_psum", bufs=4))
        ut_psum = ctx.enter_context(tc.psum_pool(name="ut_psum", bufs=2))

        grouped, codes, scales, z, y, y_t = {}, {}, {}, {}, {}, {}
        stats, rstd, shift, normed, u_t, out_sb = {}, {}, {}, {}, {}, {}

        def ok(j):
            return 0 <= j < N_BANKS

        def vector_end(j):
            return BANK if j < HEAD_BANKS else SCALAR_POS + VECTOR_POS

        def regroup_scalar(j):
            nc.scalar.copy(
                out=grouped[j][:, 0:SCALAR_POS, :],
                in_=raw_of_bank[j][:, :, 0:SCALAR_POS].rearrange("p t w -> p w t"),
            )

        def regroup_gpsimd(j):
            grouped[j] = grouped_pool.tile([P, BANK, PACK], BF16, align_bytes=64, name="grouped")
            lo = vector_end(j)
            if lo < BANK:
                nc.gpsimd.tensor_scalar(
                    out=grouped[j][:, lo:BANK, :],
                    in0=raw_of_bank[j][:, :, lo:BANK].rearrange("p t w -> p w t"),
                    scalar1=1.0,
                    scalar2=0.0,
                    op0=ALU.mult,
                    op1=ALU.add,
                )

        def regroup_vector(j):
            hi = vector_end(j)
            nc.vector.tensor_copy(
                out=grouped[j][:, SCALAR_POS:hi, :],
                in_=raw_of_bank[j][:, :, SCALAR_POS:hi].rearrange("p t w -> p w t"),
            )

        def quantise(j):
            codes[j] = quant_pool.tile([P, BANK], U32, align_bytes=64, name="codes")
            scales[j] = quant_pool.tile([P, BANK], U8, align_bytes=64, name="scales")
            nc.vector.quantize_mx(
                out=codes[j][:].bitcast(FP8X4),
                scales=scales[j][:],
                in_=grouped[j][:].rearrange("p w t -> p (w t)"),
            )

        def project(j):
            z[j] = z_psum.tile([P, BANK], F32, name="z")
            for repeat in range(PROJECT_REPEATS):
                nc.tensor.matmul_mx(
                    out=z[j][:],
                    lhsT=w_words[:].bitcast(FP4X4),
                    lhsT_scale=w_plane[:],
                    rhs=codes[j][:].bitcast(FP8X4),
                    rhs_scale=scales[j][:],
                    start=True,
                    stop=True,
                )

        def add_bias(j):
            y[j] = work_pool.tile([P, BANK], F32, name="y")
            nc.scalar.activation(out=y[j][:], in_=z[j][:], func=ACT.Identity, bias=bias_col)

        def to_positions(j):
            y_t[j] = yt_psum.tile([P, BLOCKS, BLOCK], F32, name="y_t")
            for i in range(BLOCKS):
                nc.tensor.transpose(y_t[j][:, i, :], y[j][:, i * BLOCK : (i + 1) * BLOCK], identity[:])

        def statistics(j):
            stats[j] = small_pool.tile([P, BLOCKS, 3], F32, name="stats")
            for i in range(0, BLOCKS, 2):
                nc.vector.bn_stats(
                    out=stats[j][:, i : i + 2, :].rearrange("p b f -> p (b f)"),
                    in_=y_t[j][:, i : i + 2, :].rearrange("p b c -> p c b"),
                )

        def root(j):
            rstd[j] = small_pool.tile([P, BLOCKS], F32, name="rstd")
            nc.scalar.activation(
                out=rstd[j][:], in_=stats[j][:, :, 2], func=ACT.Abs_reciprocal_sqrt, scale=1.0 / P, bias=eps_col[:]
            )

        def scale_and_shift(j):
            shift[j] = small_pool.tile([P, BLOCKS], F32, name="shift")
            nc.vector.scalar_tensor_tensor(
                out=shift[j][:], in0=stats[j][:, :, 1], scalar=-1.0, in1=rstd[j][:], op0=ALU.mult, op1=ALU.mult
            )

        def normalise(j):
            normed[j] = work_pool.tile([P, BLOCKS, BLOCK], F32, name="normed")
            for i in range(BLOCKS):
                nc.scalar.activation(
                    out=normed[j][:, i, :],
                    in_=y_t[j][:, i, :],
                    func=ACT.Identity,
                    scale=rstd[j][:, i : i + 1],
                    bias=shift[j][:, i : i + 1],
                )

        def to_channels(j):
            u_t[j] = ut_psum.tile([P, BANK], F32, name="u_t")
            for i in range(BLOCKS):
                nc.tensor.transpose(u_t[j][:, i * BLOCK : (i + 1) * BLOCK], normed[j][:, i, :], identity[:])

        def finish(j):
            b = j // BANKS_PER_IMAGE
            lo = (j % BANKS_PER_IMAGE) * BANK
            if lo == 0:
                out_sb[b] = out_pool.tile([P, POSITIONS], F32, name="out_sb")
            pieces = 2 if j == N_BANKS - 1 else 1
            width = BANK // pieces
            for piece in range(pieces):
                first = lo + piece * width
                nc.vector.scalar_tensor_tensor(
                    out=out_sb[b][:, first : first + width],
                    in0=u_t[j][:, piece * width : (piece + 1) * width],
                    scalar=gain_col,
                    in1=xn_of_image[b][:, first : first + width],
                    op0=ALU.mult,
                    op1=ALU.add,
                )
                if b == IMAGES - 1:
                    nc.sync.dma_start(out=out_view[b, :, first : first + width], in_=out_sb[b][:, first : first + width])
            if b < IMAGES - 1 and lo + BANK == POSITIONS:
                nc.sync.dma_start(out=out_view[b], in_=out_sb[b][:])

        ctx.enter_context(tc.manual_schedule())

        for j in range(3):
            regroup_gpsimd(j)
        for j in range(2):
            regroup_scalar(j)
        regroup_vector(0)

        for s in range(N_BANKS + 6):
            if ok(s):
                quantise(s)
            if ok(s - 1):
                add_bias(s - 1)
            if ok(s - 5):
                to_channels(s - 5)
            if ok(s):
                project(s)
            if ok(s - 1):
                to_positions(s - 1)
            if ok(s + 3):
                regroup_gpsimd(s + 3)
            if ok(s + 2):
                regroup_scalar(s + 2)
            if ok(s - 2):
                statistics(s - 2)
            if ok(s - 4):
                normalise(s - 4)
            if ok(s - 2):
                root(s - 2)
            if ok(s - 5):
                finish(s - 5)
            if ok(s - 3):
                scale_and_shift(s - 3)
            if s == 0:
                regroup_vector(1)
            if ok(s + 2):
                regroup_vector(s + 2)
            done = s - 5
            if ok(done) and done % BANKS_PER_IMAGE == BANKS_PER_IMAGE - 1:
                b = done // BANKS_PER_IMAGE + 2
                if b < IMAGES:
                    load_xn(b)
